import numpy as np
import ml_dtypes


def mxq(x, axis, fmt="e4m3"):
    dtype, down = {"e4m3": (ml_dtypes.float8_e4m3fn, 7), "e5m2": (ml_dtypes.float8_e5m2, 14)}[fmt]
    v = np.moveaxis(np.asarray(x, np.float32).astype(ml_dtypes.bfloat16).astype(np.float64), axis, -1)
    blocks = v.reshape(v.shape[:-1] + (-1, 32))
    amax = np.abs(blocks).max(-1, keepdims=True)
    byte = np.maximum(np.where(amax > 0, np.frexp(amax)[1] - 1 + 127, 0) - down, 1)
    scale = np.exp2(byte - 127.0)
    codes = (blocks / scale).astype(np.float32).astype(dtype).astype(np.float64)
    return np.moveaxis((codes * scale).reshape(v.shape), -1, axis)


WIDE = False


def mx_kscale(k):
    if not WIDE:
        return np.ones(k)
    levels = np.array([10, -10, 5, -5, 0])
    a = np.random.permutation(np.resize(levels, k // 512 * 4)).reshape(k // 512, 4)
    idx = np.arange(k)
    return np.exp2(a[idx // 512, idx % 128 // 32])


BF16 = ml_dtypes.bfloat16


def bf(x):
    return np.asarray(x, np.float32).astype(BF16)


def f64(x):
    return np.asarray(x).astype(np.float64)


B, N, DIM, H, DK, DV, KB = 1, 1024, 1024, 8, 16, 64, 512
WT = 256.0
EPS = 1e-12
DI = H * (DK + DV)


def l2norm(t):
    n = np.sqrt((t * t).sum(-1, keepdims=True))
    return t / np.maximum(n, EPS)


def setup_inputs():
    s = mx_kscale(DIM)
    return {'tokens': bf(np.random.standard_normal((B, N, DIM)) * s),
            'w_qg': bf(np.random.standard_normal((DI, DIM)) / np.sqrt(DIM) / s[None, :]),
            'w_kv': bf(np.random.standard_normal((DI, DIM)) / np.sqrt(DIM) / s[None, :]),
            'sm_log': bf(np.linspace(3.0, 5.8, H) + 0.1 * np.random.standard_normal(H))}


def reference(tokens, w_qg, w_kv, sm_log):
    tq = mxq(f64(tokens), 2, 'e4m3')
    qg = (tq @ mxq(f64(w_qg), 1, 'e4m3').T).reshape(B, N, H, DK + DV).transpose(0, 2, 1, 3)
    kv = (tq @ mxq(f64(w_kv), 1, 'e4m3').T).reshape(B, N, H, DK + DV).transpose(0, 2, 1, 3)
    q, g = qg[..., :DK], qg[..., DK:]
    k, v = kv[..., :DK], kv[..., DK:]
    q, k, v = l2norm(q), l2norm(k), l2norm(v)
    w = np.exp(f64(sm_log)) + 1.0
    gamma = np.where(w < WT, 0.5 * (np.cos(np.pi * w / WT) + 1.0), 0.0)
    freq = np.pi * gamma / w
    ang = freq[:, None] * np.arange(N, dtype=np.float64)[None, :]
    cos = np.cos(ang)[None, :, :, None]
    sin = np.sin(ang)[None, :, :, None]

    def rotate(t):
        x0, x1 = t[..., 0:1], t[..., 1:2]
        return np.concatenate([x0 * cos - x1 * sin, x0 * sin + x1 * cos, t[..., 2:]], axis=-1)

    gate = np.tanh(g / (1.0 + np.exp(-g)))
    return rotate(q), gate, rotate(k), v

@@ -1,0 +1,301 @@
+import math
+from contextlib import ExitStack
+
+import concourse.masks as masks
+import concourse.mybir as mybir
+
+F32 = mybir.dt.float32
+BF16 = mybir.dt.bfloat16
+I32 = mybir.dt.int32
+U32 = mybir.dt.uint32
+U8 = mybir.dt.uint8
+FP8X4 = mybir.dt.float8_e4m3fn_x4
+ACT = mybir.ActivationFunctionType
+ALU = mybir.AluOpType
+
+P = 128
+N_TOK, DIM, H, DK, DV = 1024, 1024, 8, 16, 64
+HC = DK + DV
+T = N_TOK // P
+PAIRS = T // 2
+HALF = T // 2
+K_PASS = 4 * P
+PASSES = DIM // K_PASS
+BANK = 512
+VJ = DV // DK
+WINDOW = 256.0
+EPS = 1e-12
+ROUND = 1.5 * 2.0**23
+
+FLOPS = 2 * N_TOK * DIM * 2 * H * HC
+
+
+def tile_gatedscreeningtile_pa_kernel(
+    tc, tokens, w_qg, w_kv, sm_log, out_0, out_1, out_2, out_3
+):
+    nc = tc.nc
+    with ExitStack() as ctx:
+        keep = ctx.enter_context(tc.tile_pool(name="keep", bufs=1))
+        work = ctx.enter_context(tc.tile_pool(name="work", bufs=2))
+        psum = ctx.enter_context(tc.psum_pool(name="psum", bufs=8))
+        ctx.enter_context(tc.manual_schedule())
+
+        def head_rows(w, first, count):
+            rows = w.rearrange("(h c) k -> h c k", c=HC)[:, first : first + count, :]
+            return rows.rearrange("h (dd j) k -> dd h (j k)", dd=DK)
+
+        log_window = keep.tile([P, H], BF16, name="log_window")
+        nc.scalar.dma_start(out=log_window[:], in_=sm_log.partition_broadcast(P))
+        g_rows = keep.tile([P, VJ * DIM], BF16, name="g_rows")
+        nc.sync.dma_start(out=g_rows[:], in_=head_rows(w_qg, DK, DV))
+        tok_rows = keep.tile([P, T * DIM], BF16, name="tok_rows")
+        tok_dram = tokens.rearrange("b (p t) k -> (b p) (t k)", t=T)
+        for a in range(PAIRS):
+            cols = slice(2 * a * DIM, 2 * (a + 1) * DIM)
+            nc.sync.dma_start(out=tok_rows[:, cols], in_=tok_dram[:, cols])
+        v_rows = keep.tile([P, VJ * DIM], BF16, name="v_rows")
+        nc.sync.dma_start(out=v_rows[:], in_=head_rows(w_kv, DK, DV))
+        qk_rows = keep.tile([P, 2 * DIM], BF16, name="qk_rows")
+        nc.sync.dma_start(out=qk_rows[:, 0:DIM], in_=head_rows(w_qg, 0, DK))
+        nc.sync.dma_start(out=qk_rows[:, DIM : 2 * DIM], in_=head_rows(w_kv, 0, DK))
+
+        ident = keep.tile([P, P], F32, name="ident")
+        masks.make_identity(nc, ident[:])
+
+        pos_int = keep.tile([P, T], I32, name="pos_int")
+        nc.gpsimd.iota(pos_int[:], pattern=[[1, T]], base=0, channel_multiplier=T)
+        pos = keep.tile([P, T], F32, name="pos")
+        nc.vector.tensor_copy(out=pos[:], in_=pos_int[:])
+        inv_w = keep.tile([P, H], F32, name="inv_w")
+        nc.scalar.activation(out=inv_w[:], in_=log_window[:], func=ACT.Sigmoid, scale=-1.0)
+        window = keep.tile([P, H], F32, name="window")
+        nc.vector.reciprocal(out=window[:], in_=inv_w[:])
+        below = keep.tile([P, H], F32, name="below")
+        nc.vector.tensor_scalar(
+            out=below[:], in0=window[:], scalar1=WINDOW, scalar2=WINDOW, op0=ALU.min, op1=ALU.subtract
+        )
+        root_gamma = keep.tile([P, H], F32, name="root_gamma")
+        nc.scalar.activation(
+            out=root_gamma[:], in_=below[:], func=ACT.Sin, scale=math.pi / (2.0 * WINDOW)
+        )
+        half_gamma = keep.tile([P, H], F32, name="half_gamma")
+        nc.vector.scalar_tensor_tensor(
+            out=half_gamma[:], in0=root_gamma[:], scalar=0.5, in1=root_gamma[:], op0=ALU.mult, op1=ALU.mult
+        )
+        turns_per_pos = keep.tile([P, H], F32, name="turns_per_pos")
+        nc.vector.tensor_tensor(out=turns_per_pos[:], in0=half_gamma[:], in1=inv_w[:], op=ALU.mult)
+        turns = keep.tile([P, H, T], F32, name="turns")
+        nc.vector.tensor_tensor(
+            out=turns[:],
+            in0=turns_per_pos[:].unsqueeze(2).to_broadcast([P, H, T]),
+            in1=pos[:].unsqueeze(1).to_broadcast([P, H, T]),
+            op=ALU.mult,
+        )
+        whole = keep.tile([P, H, T], F32, name="whole")
+        nc.vector.tensor_scalar(
+            out=whole[:], in0=turns[:], scalar1=ROUND, scalar2=ROUND, op0=ALU.add, op1=ALU.subtract
+        )
+        frac = keep.tile([P, H, T], F32, name="frac")
+        nc.vector.tensor_tensor(out=frac[:], in0=turns[:], in1=whole[:], op=ALU.subtract)
+        size = keep.tile([P, H, T], F32, name="size")
+        nc.vector.scalar_tensor_tensor(
+            out=size[:], in0=frac[:], scalar=-1.0, in1=frac[:], op0=ALU.mult, op1=ALU.max
+        )
+        lead = keep.tile([P, H, T], F32, name="lead")
+        nc.vector.tensor_scalar(
+            out=lead[:], in0=size[:], scalar1=-1.0, scalar2=0.25, op0=ALU.mult, op1=ALU.add
+        )
+        sin_t = keep.tile([P, H, T], F32, name="sin_t")
+        nc.scalar.activation(out=sin_t[:], in_=frac[:], func=ACT.Sin, scale=2.0 * math.pi)
+        cos_t = keep.tile([P, H, T], F32, name="cos_t")
+        nc.scalar.activation(out=cos_t[:], in_=lead[:], func=ACT.Sin, scale=2.0 * math.pi)
+
+        def mx_operand(name, columns):
+            grouped = keep.tile([P, PASSES * columns * 4], BF16, name=name + "_grouped", align_bytes=64)
+            codes = keep.tile([P, PASSES * columns], U32, name=name + "_codes", align_bytes=64)
+            scales = keep.tile([P, PASSES * columns], U8, name=name + "_scales", align_bytes=64)
+            return grouped, codes, scales
+
+        def flip(rows, tile_index, copy, grouped_words):
+            words = rows[:].bitcast(F32)
+            bank = psum.tile([P, BANK], F32, tag="bank", name="flipped")
+            for c in range(BANK // P):
+                src = tile_index * BANK + c * P
+                nc.tensor.transpose(bank[:, c * P : (c + 1) * P], words[:, src : src + P], ident[:])
+            copy(out=grouped_words, in_=bank[:].rearrange("p (g u r) -> p g r u", g=PASSES, u=2))
+
+        def quantise(grouped, codes, scales, first, count):
+            nc.vector.quantize_mx(
+                out=codes[:, first : first + count].bitcast(FP8X4),
+                scales=scales[:, first : first + count],
+                in_=grouped[:, 4 * first : 4 * (first + count)],
+            )
+
+        def copier(index, scalar_helps):
+            return nc.scalar.copy if scalar_helps and index % 2 == 0 else nc.vector.tensor_copy
+
+        def prepare_weights(rows, operand, tiles, scalar_helps):
+            grouped, codes, scales = operand
+            words = grouped[:].bitcast(F32).rearrange("p (g c u) -> p g c u", g=PASSES, u=2)
+            for j in range(tiles):
+                flip(rows, j, copier(j, scalar_helps), words[:, :, j * P : (j + 1) * P, :])
+            quantise(grouped, codes, scales, 0, PASSES * tiles * P)
+
+        tok = mx_operand("tok", T * P)
+
+        def prepare_tokens(a, scalar_helps):
+            grouped, codes, scales = tok
+            words = grouped[:].bitcast(F32).rearrange("p (t g r u) -> p t g r u", t=T, g=PASSES, u=2)
+            for t in (2 * a, 2 * a + 1):
+                flip(tok_rows, t, copier(t, scalar_helps), words[:, t])
+            quantise(grouped, codes, scales, 2 * a * PASSES * P, 2 * PASSES * P)
+
+        def project(acc, t, operand, columns):
+            codes, scales = operand[1], operand[2]
+            for g in range(PASSES):
+                lhs = slice((t * PASSES + g) * P, (t * PASSES + g + 1) * P)
+                rhs = slice(g * columns, (g + 1) * columns)
+                nc.tensor.matmul_mx(
+                    out=acc,
+                    lhsT=tok[1][:, lhs].bitcast(FP8X4),
+                    lhsT_scale=tok[2][:, lhs],
+                    rhs=codes[:, rhs].bitcast(FP8X4),
+                    rhs_scale=scales[:, rhs],
+                    start=(g == 0),
+                    stop=(g == PASSES - 1),
+                )
+
+        def in_bank(bank):
+            return bank[:].rearrange("p (j dd h) -> p h dd j", j=VJ, dd=DK)
+
+        def in_output(values):
+            return values.rearrange("p h (dd j) -> p h dd j", j=VJ)
+
+        def hbm(out):
+            return out.rearrange("b h (p t) d -> p (b h) t d", t=T)
+
+        g_op = mx_operand("g", VJ * P)
+        v_op = mx_operand("v", VJ * P)
+        qk_op = mx_operand("qk", 2 * P)
+        gate = keep.tile([P, H, T, DV], F32, name="gate")
+
+        def gate_pair(a):
+            for t in (2 * a, 2 * a + 1):
+                acc = psum.tile([P, BANK], F32, tag="bank", name="g_acc")
+                project(acc[:], t, g_op, VJ * P)
+                nc.scalar.activation(out=in_output(gate[:, :, t, :]), in_=in_bank(acc), func=ACT.Silu)
+            if a % 2 == 1:
+                done = slice(2 * a + 2 - HALF, 2 * a + 2)
+                nc.scalar.activation(out=gate[:, :, done, :], in_=gate[:, :, done, :], func=ACT.Tanh)
+                nc.sync.dma_start(out=hbm(out_1)[:, :, done, :], in_=gate[:, :, done, :])
+
+        prepare_weights(g_rows, g_op, VJ, True)
+        prepare_tokens(0, True)
+        for a in range(PAIRS):
+            if a + 1 < PAIRS:
+                prepare_tokens(a + 1, False)
+            else:
+                prepare_weights(v_rows, v_op, VJ, False)
+            gate_pair(a)
+        prepare_weights(qk_rows, qk_op, 2, False)
+
+        qk_out = keep.tile([P, 2, H, T, DK], F32, name="qk_out")
+        v_out = keep.tile([P, H, T, DV], F32, name="v_out")
+        N_QK = 2 * 2 * H
+        N_V = 2 * H
+        live = {}
+
+        def start_pair(a):
+            qk_acc = psum.tile([P, BANK], F32, tag="bank", name="qk_acc")
+            for i in range(2):
+                project(qk_acc[:, i * 2 * P : (i + 1) * 2 * P], 2 * a + i, qk_op, 2 * P)
+            v_acc = []
+            for i in range(2):
+                acc = psum.tile([P, BANK], F32, tag="bank", name="v_acc")
+                project(acc[:], 2 * a + i, v_op, VJ * P)
+                v_acc.append(acc)
+            sums = work.tile([P, N_QK + N_V], F32, name="sums")
+            qk_sq = work.tile([P, N_QK, DK], F32, name="qk_sq")
+            nc.scalar.activation(
+                out=qk_sq[:].rearrange("p (e h) dd -> p e h dd", h=H),
+                in_=qk_acc[:].rearrange("p (e dd h) -> p e h dd", dd=DK, h=H),
+                func=ACT.Square,
+            )
+            nc.vector.tensor_reduce(
+                out=sums[:, 0:N_QK], in_=qk_sq[:], axis=mybir.AxisListType.X, op=ALU.add
+            )
+            v_sq = work.tile([P, N_V, DV], F32, name="v_sq")
+            for i in range(2):
+                by_head = v_acc[i][:].rearrange("p (m h) -> p h m", h=H)
+                for h in range(H):
+                    e = i * H + h
+                    nc.scalar.activation(
+                        out=v_sq[:, e, :],
+                        in_=by_head[:, h, :],
+                        func=ACT.Square,
+                        accum_out=sums[:, N_QK + e : N_QK + e + 1],
+                    )
+            live[a] = (qk_acc, v_acc, sums)
+
+        def floor_sums(a):
+            sums = live[a][2]
+            floored = work.tile([P, N_QK + N_V], F32, name="floored")
+            nc.vector.tensor_scalar_max(out=floored[:], in0=sums[:], scalar1=EPS * EPS)
+            return floored
+
+        def finish_pair(a, floored):
+            qk_acc, v_acc, sums = live[a]
+            norm = work.tile([P, N_QK + N_V], F32, name="norm")
+            nc.scalar.activation(out=norm[:], in_=floored[:], func=ACT.Sqrt)
+            inv = work.tile([P, N_QK + N_V], F32, name="inv")
+            nc.vector.reciprocal(out=inv[:], in_=norm[:])
+            both = slice(2 * a, 2 * a + 2)
+            for s in range(2):
+                nc.vector.tensor_tensor(
+                    out=qk_out[:, s, :, both, :],
+                    in0=qk_acc[:].rearrange("p (i s dd h) -> p s h i dd", i=2, s=2, dd=DK)[:, s],
+                    in1=inv[:, 0:N_QK]
+                    .rearrange("p (i s h) -> p s h i", i=2, s=2)[:, s]
+                    .unsqueeze(3)
+                    .to_broadcast([P, H, 2, DK]),
+                    op=ALU.mult,
+                )
+            for i in range(2):
+                first = N_QK + i * H
+                nc.vector.tensor_tensor(
+                    out=in_output(v_out[:, :, 2 * a + i, :]),
+                    in0=in_bank(v_acc[i]),
+                    in1=inv[:, first : first + H].unsqueeze(2).unsqueeze(3).to_broadcast([P, H, DK, VJ]),
+                    op=ALU.mult,
+                )
+
+        def rotate_and_store(done):
+            nc.sync.dma_start(out=hbm(out_3)[:, :, done, :], in_=v_out[:, :, done, :])
+            x0 = qk_out[:, :, :, done, 0]
+            x1 = qk_out[:, :, :, done, 1]
+            shape = [P, 2, H, HALF]
+            cos = cos_t[:, :, done].unsqueeze(1).to_broadcast(shape)
+            sin = sin_t[:, :, done].unsqueeze(1).to_broadcast(shape)
+            x0_cos = work.tile(shape, F32, name="x0_cos")
+            x1_sin = work.tile(shape, F32, name="x1_sin")
+            x0_sin = work.tile(shape, F32, name="x0_sin")
+            x1_cos = work.tile(shape, F32, name="x1_cos")
+            nc.vector.tensor_tensor(out=x0_cos[:], in0=x0, in1=cos, op=ALU.mult)
+            nc.vector.tensor_tensor(out=x1_sin[:], in0=x1, in1=sin, op=ALU.mult)
+            nc.vector.tensor_tensor(out=x0_sin[:], in0=x0, in1=sin, op=ALU.mult)
+            nc.vector.tensor_tensor(out=x1_cos[:], in0=x1, in1=cos, op=ALU.mult)
+            nc.vector.tensor_tensor(out=x0, in0=x0_cos[:], in1=x1_sin[:], op=ALU.subtract)
+            nc.vector.tensor_tensor(out=x1, in0=x0_sin[:], in1=x1_cos[:], op=ALU.add)
+            nc.sync.dma_start(out=hbm(out_0)[:, :, done, :], in_=qk_out[:, 0, :, done, :])
+            nc.sync.dma_start(out=hbm(out_2)[:, :, done, :], in_=qk_out[:, 1, :, done, :])
+
+        floored = {}
+        for a in range(PAIRS + 1):
+            if a < PAIRS:
+                start_pair(a)
+            if a > 0:
+                finish_pair(a - 1, floored[a - 1])
+                if a % 2 == 0:
+                    rotate_and_store(slice(2 * a - HALF, 2 * a))
+            if a < PAIRS:
+                floored[a] = floor_sums(a)

@@ -203,74 +203,76 @@ def tile_gatedscreeningtile_pa_kernel(
         v_out = keep.tile([P, H, T, DV], F32, name="v_out")
         N_QK = 2 * 2 * H
         N_V = 2 * H
-        live = {}
+        qk_acc, v_acc, sums, inv = {}, {}, {}, {}
 
-        def start_pair(a):
-            qk_acc = psum.tile([P, BANK], F32, tag="bank", name="qk_acc")
+        def products(a):
+            qk_acc[a] = psum.tile([P, BANK], F32, tag="bank", name="qk_acc")
             for i in range(2):
-                project(qk_acc[:, i * 2 * P : (i + 1) * 2 * P], 2 * a + i, qk_op, 2 * P)
-            v_acc = []
+                project(qk_acc[a][:, i * 2 * P : (i + 1) * 2 * P], 2 * a + i, qk_op, 2 * P)
             for i in range(2):
-                acc = psum.tile([P, BANK], F32, tag="bank", name="v_acc")
-                project(acc[:], 2 * a + i, v_op, VJ * P)
-                v_acc.append(acc)
-            sums = work.tile([P, N_QK + N_V], F32, name="sums")
+                v_acc[a, i] = psum.tile([P, BANK], F32, tag="bank", name="v_acc")
+                project(v_acc[a, i][:], 2 * a + i, v_op, VJ * P)
+            sums[a] = work.tile([P, N_QK + N_V], F32, name="sums")
+
+        def sum_squares_qk(a):
             qk_sq = work.tile([P, N_QK, DK], F32, name="qk_sq")
             nc.scalar.activation(
                 out=qk_sq[:].rearrange("p (e h) dd -> p e h dd", h=H),
-                in_=qk_acc[:].rearrange("p (e dd h) -> p e h dd", dd=DK, h=H),
+                in_=qk_acc[a][:].rearrange("p (e dd h) -> p e h dd", dd=DK, h=H),
                 func=ACT.Square,
             )
             nc.vector.tensor_reduce(
-                out=sums[:, 0:N_QK], in_=qk_sq[:], axis=mybir.AxisListType.X, op=ALU.add
+                out=sums[a][:, 0:N_QK], in_=qk_sq[:], axis=mybir.AxisListType.X, op=ALU.add
             )
+
+        def sum_squares_v(a):
             v_sq = work.tile([P, N_V, DV], F32, name="v_sq")
             for i in range(2):
-                by_head = v_acc[i][:].rearrange("p (m h) -> p h m", h=H)
+                by_head = v_acc[a, i][:].rearrange("p (m h) -> p h m", h=H)
                 for h in range(H):
                     e = i * H + h
                     nc.scalar.activation(
                         out=v_sq[:, e, :],
                         in_=by_head[:, h, :],
                         func=ACT.Square,
-                        accum_out=sums[:, N_QK + e : N_QK + e + 1],
+                        accum_out=sums[a][:, N_QK + e : N_QK + e + 1],
                     )
-            live[a] = (qk_acc, v_acc, sums)
 
         def floor_sums(a):
-            sums = live[a][2]
             floored = work.tile([P, N_QK + N_V], F32, name="floored")
-            nc.vector.tensor_scalar_max(out=floored[:], in0=sums[:], scalar1=EPS * EPS)
+            nc.vector.tensor_scalar_max(out=floored[:], in0=sums[a][:], scalar1=EPS * EPS)
             return floored
 
-        def finish_pair(a, floored):
-            qk_acc, v_acc, sums = live[a]
-            norm = work.tile([P, N_QK + N_V], F32, name="norm")
-            nc.scalar.activation(out=norm[:], in_=floored[:], func=ACT.Sqrt)
-            inv = work.tile([P, N_QK + N_V], F32, name="inv")
-            nc.vector.reciprocal(out=inv[:], in_=norm[:])
+        def invert_norms(a, floored):
+            inv[a] = work.tile([P, N_QK + N_V], F32, name="inv")
+            nc.scalar.activation(out=inv[a][:], in_=floored[:], func=ACT.Abs_reciprocal_sqrt)
+
+        def scale_qk(a):
             both = slice(2 * a, 2 * a + 2)
             for s in range(2):
                 nc.vector.tensor_tensor(
                     out=qk_out[:, s, :, both, :],
-                    in0=qk_acc[:].rearrange("p (i s dd h) -> p s h i dd", i=2, s=2, dd=DK)[:, s],
-                    in1=inv[:, 0:N_QK]
+                    in0=qk_acc[a][:].rearrange("p (i s dd h) -> p s h i dd", i=2, s=2, dd=DK)[:, s],
+                    in1=inv[a][:, 0:N_QK]
                     .rearrange("p (i s h) -> p s h i", i=2, s=2)[:, s]
                     .unsqueeze(3)
                     .to_broadcast([P, H, 2, DK]),
                     op=ALU.mult,
                 )
+
+        def scale_v(a):
             for i in range(2):
                 first = N_QK + i * H
                 nc.vector.tensor_tensor(
                     out=in_output(v_out[:, :, 2 * a + i, :]),
-                    in0=in_bank(v_acc[i]),
-                    in1=inv[:, first : first + H].unsqueeze(2).unsqueeze(3).to_broadcast([P, H, DK, VJ]),
+                    in0=in_bank(v_acc[a, i]),
+                    in1=inv[a][:, first : first + H].unsqueeze(2).unsqueeze(3).to_broadcast([P, H, DK, VJ]),
                     op=ALU.mult,
                 )
+            both = slice(2 * a, 2 * a + 2)
+            nc.sync.dma_start(out=hbm(out_3)[:, :, both, :], in_=v_out[:, :, both, :])
 
-        def rotate_and_store(done):
-            nc.sync.dma_start(out=hbm(out_3)[:, :, done, :], in_=v_out[:, :, done, :])
+        def rotate(done):
             x0 = qk_out[:, :, :, done, 0]
             x1 = qk_out[:, :, :, done, 1]
             shape = [P, 2, H, HALF]
@@ -289,13 +291,17 @@ def tile_gatedscreeningtile_pa_kernel(
             nc.sync.dma_start(out=hbm(out_0)[:, :, done, :], in_=qk_out[:, 0, :, done, :])
             nc.sync.dma_start(out=hbm(out_2)[:, :, done, :], in_=qk_out[:, 1, :, done, :])
 
-        floored = {}
-        for a in range(PAIRS + 1):
-            if a < PAIRS:
-                start_pair(a)
-            if a > 0:
-                finish_pair(a - 1, floored[a - 1])
-                if a % 2 == 0:
-                    rotate_and_store(slice(2 * a - HALF, 2 * a))
-            if a < PAIRS:
-                floored[a] = floor_sums(a)
+        products(0)
+        sum_squares_qk(0)
+        for a in range(PAIRS):
+            if a + 1 < PAIRS:
+                products(a + 1)
+            sum_squares_v(a)
+            floored = floor_sums(a)
+            if a + 1 < PAIRS:
+                sum_squares_qk(a + 1)
+            invert_norms(a, floored)
+            scale_qk(a)
+            if a % 2 == 1:
+                rotate(slice(2 * a + 2 - HALF, 2 * a + 2))
+            scale_v(a)

@@ -36,36 +36,43 @@ def tile_gatedscreeningtile_pa_kernel(
     nc = tc.nc
     with ExitStack() as ctx:
         keep = ctx.enter_context(tc.tile_pool(name="keep", bufs=1))
-        work = ctx.enter_context(tc.tile_pool(name="work", bufs=2))
         psum = ctx.enter_context(tc.psum_pool(name="psum", bufs=8))
         ctx.enter_context(tc.manual_schedule())
 
-        def head_rows(w, first, count):
-            rows = w.rearrange("(h c) k -> h c k", c=HC)[:, first : first + count, :]
-            return rows.rearrange("h (dd j) k -> dd h (j k)", dd=DK)
+        def mx_operand(name, columns):
+            grouped = keep.tile([P, PASSES * columns * 4], BF16, name=name + "_grouped", align_bytes=64)
+            codes = keep.tile([P, PASSES * columns], U32, name=name + "_codes", align_bytes=64)
+            scales = keep.tile([P, PASSES * columns], U8, name=name + "_scales", align_bytes=64)
+            return grouped, codes, scales, columns
+
+        def head_rows(w, first):
+            return w.rearrange("(h c) k -> c h k", c=HC)[first : first + DK]
+
+        tok_op = mx_operand("tok", T * P)
+        g_op = mx_operand("g", VJ * P)
+        qk_op = mx_operand("qk", 2 * P)
+        v_op = mx_operand("v", VJ * P)
+        token_tiles = tokens.rearrange("b (p t) k -> t (b p) k", t=T)
+        row_tiles = (
+            [(g_op, j, head_rows(w_qg, DK + j * DK)) for j in range(VJ)]
+            + [(tok_op, t, token_tiles[t]) for t in range(T)]
+            + [(qk_op, 0, head_rows(w_qg, 0)), (qk_op, 1, head_rows(w_kv, 0))]
+            + [(v_op, j, head_rows(w_kv, DK + j * DK)) for j in range(VJ)]
+        )
 
         log_window = keep.tile([P, H], BF16, name="log_window")
         nc.scalar.dma_start(out=log_window[:], in_=sm_log.partition_broadcast(P))
-        g_rows = keep.tile([P, VJ * DIM], BF16, name="g_rows")
-        nc.sync.dma_start(out=g_rows[:], in_=head_rows(w_qg, DK, DV))
-        tok_rows = keep.tile([P, T * DIM], BF16, name="tok_rows")
-        tok_dram = tokens.rearrange("b (p t) k -> (b p) (t k)", t=T)
-        for a in range(PAIRS):
-            cols = slice(2 * a * DIM, 2 * (a + 1) * DIM)
-            nc.sync.dma_start(out=tok_rows[:, cols], in_=tok_dram[:, cols])
-        v_rows = keep.tile([P, VJ * DIM], BF16, name="v_rows")
-        nc.sync.dma_start(out=v_rows[:], in_=head_rows(w_kv, DK, DV))
-        qk_rows = keep.tile([P, 2 * DIM], BF16, name="qk_rows")
-        nc.sync.dma_start(out=qk_rows[:, 0:DIM], in_=head_rows(w_qg, 0, DK))
-        nc.sync.dma_start(out=qk_rows[:, DIM : 2 * DIM], in_=head_rows(w_kv, 0, DK))
+        rows = keep.tile([P, len(row_tiles) * DIM], BF16, name="rows")
+        for n in range(len(row_tiles)):
+            nc.sync.dma_start(out=rows[:, n * DIM : (n + 1) * DIM], in_=row_tiles[n][2])
 
         ident = keep.tile([P, P], F32, name="ident")
         masks.make_identity(nc, ident[:])
 
         pos_int = keep.tile([P, T], I32, name="pos_int")
         nc.gpsimd.iota(pos_int[:], pattern=[[1, T]], base=0, channel_multiplier=T)
-        pos = keep.tile([P, T], F32, name="pos")
-        nc.vector.tensor_copy(out=pos[:], in_=pos_int[:])
+        half_pos = keep.tile([P, T], F32, name="half_pos")
+        nc.vector.tensor_scalar_mul(out=half_pos[:], in0=pos_int[:], scalar1=0.5)
         inv_w = keep.tile([P, H], F32, name="inv_w")
         nc.scalar.activation(out=inv_w[:], in_=log_window[:], func=ACT.Sigmoid, scale=-1.0)
         window = keep.tile([P, H], F32, name="window")
@@ -78,174 +85,127 @@ def tile_gatedscreeningtile_pa_kernel(
         nc.scalar.activation(
             out=root_gamma[:], in_=below[:], func=ACT.Sin, scale=math.pi / (2.0 * WINDOW)
         )
-        half_gamma = keep.tile([P, H], F32, name="half_gamma")
-        nc.vector.scalar_tensor_tensor(
-            out=half_gamma[:], in0=root_gamma[:], scalar=0.5, in1=root_gamma[:], op0=ALU.mult, op1=ALU.mult
-        )
-        turns_per_pos = keep.tile([P, H], F32, name="turns_per_pos")
-        nc.vector.tensor_tensor(out=turns_per_pos[:], in0=half_gamma[:], in1=inv_w[:], op=ALU.mult)
+        gamma = keep.tile([P, H], F32, name="gamma")
+        nc.gpsimd.tensor_tensor(out=gamma[:], in0=root_gamma[:], in1=root_gamma[:], op=ALU.mult)
+        gamma_by_w = keep.tile([P, H], F32, name="gamma_by_w")
+        nc.gpsimd.tensor_tensor(out=gamma_by_w[:], in0=gamma[:], in1=inv_w[:], op=ALU.mult)
         turns = keep.tile([P, H, T], F32, name="turns")
-        nc.vector.tensor_tensor(
+        nc.gpsimd.tensor_tensor(
             out=turns[:],
-            in0=turns_per_pos[:].unsqueeze(2).to_broadcast([P, H, T]),
-            in1=pos[:].unsqueeze(1).to_broadcast([P, H, T]),
+            in0=gamma_by_w[:].unsqueeze(2).to_broadcast([P, H, T]),
+            in1=half_pos[:].unsqueeze(1).to_broadcast([P, H, T]),
             op=ALU.mult,
         )
         whole = keep.tile([P, H, T], F32, name="whole")
-        nc.vector.tensor_scalar(
+        nc.gpsimd.tensor_scalar(
             out=whole[:], in0=turns[:], scalar1=ROUND, scalar2=ROUND, op0=ALU.add, op1=ALU.subtract
         )
         frac = keep.tile([P, H, T], F32, name="frac")
-        nc.vector.tensor_tensor(out=frac[:], in0=turns[:], in1=whole[:], op=ALU.subtract)
-        size = keep.tile([P, H, T], F32, name="size")
-        nc.vector.scalar_tensor_tensor(
-            out=size[:], in0=frac[:], scalar=-1.0, in1=frac[:], op0=ALU.mult, op1=ALU.max
-        )
-        lead = keep.tile([P, H, T], F32, name="lead")
-        nc.vector.tensor_scalar(
-            out=lead[:], in0=size[:], scalar1=-1.0, scalar2=0.25, op0=ALU.mult, op1=ALU.add
-        )
+        nc.gpsimd.tensor_tensor(out=frac[:], in0=turns[:], in1=whole[:], op=ALU.subtract)
         sin_t = keep.tile([P, H, T], F32, name="sin_t")
-        nc.scalar.activation(out=sin_t[:], in_=frac[:], func=ACT.Sin, scale=2.0 * math.pi)
         cos_t = keep.tile([P, H, T], F32, name="cos_t")
-        nc.scalar.activation(out=cos_t[:], in_=lead[:], func=ACT.Sin, scale=2.0 * math.pi)
 
-        def mx_operand(name, columns):
-            grouped = keep.tile([P, PASSES * columns * 4], BF16, name=name + "_grouped", align_bytes=64)
-            codes = keep.tile([P, PASSES * columns], U32, name=name + "_codes", align_bytes=64)
-            scales = keep.tile([P, PASSES * columns], U8, name=name + "_scales", align_bytes=64)
-            return grouped, codes, scales
-
-        def flip(rows, tile_index, copy, grouped_words):
-            words = rows[:].bitcast(F32)
-            bank = psum.tile([P, BANK], F32, tag="bank", name="flipped")
-            for c in range(BANK // P):
-                src = tile_index * BANK + c * P
-                nc.tensor.transpose(bank[:, c * P : (c + 1) * P], words[:, src : src + P], ident[:])
-            copy(out=grouped_words, in_=bank[:].rearrange("p (g u r) -> p g r u", g=PASSES, u=2))
-
-        def quantise(grouped, codes, scales, first, count):
-            nc.vector.quantize_mx(
-                out=codes[:, first : first + count].bitcast(FP8X4),
-                scales=scales[:, first : first + count],
-                in_=grouped[:, 4 * first : 4 * (first + count)],
+        def sines():
+            nc.scalar.activation(out=sin_t[:], in_=frac[:], func=ACT.Sin, scale=2.0 * math.pi)
+            half_sin = keep.tile([P, H, T], F32, name="half_sin")
+            nc.scalar.activation(out=half_sin[:], in_=frac[:], func=ACT.Sin, scale=math.pi)
+            half_sq = keep.tile([P, H, T], F32, name="half_sq")
+            nc.gpsimd.tensor_tensor(out=half_sq[:], in0=half_sin[:], in1=half_sin[:], op=ALU.mult)
+            nc.gpsimd.tensor_scalar(
+                out=cos_t[:], in0=half_sq[:], scalar1=-2.0, scalar2=1.0, op0=ALU.mult, op1=ALU.add
             )
 
-        def copier(index, scalar_helps):
-            return nc.scalar.copy if scalar_helps and index % 2 == 0 else nc.vector.tensor_copy
+        FIRST = VJ + HALF + 1
+        AHEAD = 3
 
-        def prepare_weights(rows, operand, tiles, scalar_helps):
-            grouped, codes, scales = operand
-            words = grouped[:].bitcast(F32).rearrange("p (g c u) -> p g c u", g=PASSES, u=2)
-            for j in range(tiles):
-                flip(rows, j, copier(j, scalar_helps), words[:, :, j * P : (j + 1) * P, :])
-            quantise(grouped, codes, scales, 0, PASSES * tiles * P)
+        def flip(n):
+            operand, j = row_tiles[n][0], row_tiles[n][1]
+            words = rows[:].bitcast(F32)[:, n * BANK : (n + 1) * BANK]
+            bank = psum.tile([P, BANK], F32, tag="bank", name="flipped")
+            for c in range(BANK // P):
+                nc.tensor.transpose(bank[:, c * P : (c + 1) * P], words[:, c * P : (c + 1) * P], ident[:])
+            grouped = operand[0][:].bitcast(F32).rearrange("p (g c u) -> p g c u", g=PASSES, u=2)
+            copy = nc.scalar.copy if n < FIRST and n % 2 == 1 else nc.vector.tensor_copy
+            copy(
+                out=grouped[:, :, j * P : (j + 1) * P, :],
+                in_=bank[:].rearrange("p (g u r) -> p g r u", g=PASSES, u=2),
+            )
 
-        tok = mx_operand("tok", T * P)
-
-        def prepare_tokens(a, scalar_helps):
-            grouped, codes, scales = tok
-            words = grouped[:].bitcast(F32).rearrange("p (t g r u) -> p t g r u", t=T, g=PASSES, u=2)
-            for t in (2 * a, 2 * a + 1):
-                flip(tok_rows, t, copier(t, scalar_helps), words[:, t])
-            quantise(grouped, codes, scales, 2 * a * PASSES * P, 2 * PASSES * P)
-
-        def project(acc, t, operand, columns):
-            codes, scales = operand[1], operand[2]
+        def quantise(n):
+            (grouped, codes, scales, columns), j = row_tiles[n][0], row_tiles[n][1]
             for g in range(PASSES):
-                lhs = slice((t * PASSES + g) * P, (t * PASSES + g + 1) * P)
+                first = g * columns + j * P
+                nc.vector.quantize_mx(
+                    out=codes[:, first : first + P].bitcast(FP8X4),
+                    scales=scales[:, first : first + P],
+                    in_=grouped[:, 4 * first : 4 * (first + P)],
+                )
+
+        def prepare(first, count):
+            for n in range(first, first + count):
+                flip(n)
+                if n > 0:
+                    quantise(n - 1)
+
+        def project(acc, t, operand):
+            codes, scales, columns = operand[1], operand[2], operand[3]
+            for g in range(PASSES):
+                lhs = slice(g * N_TOK + t * P, g * N_TOK + (t + 1) * P)
                 rhs = slice(g * columns, (g + 1) * columns)
                 nc.tensor.matmul_mx(
                     out=acc,
-                    lhsT=tok[1][:, lhs].bitcast(FP8X4),
-                    lhsT_scale=tok[2][:, lhs],
+                    lhsT=tok_op[1][:, lhs].bitcast(FP8X4),
+                    lhsT_scale=tok_op[2][:, lhs],
                     rhs=codes[:, rhs].bitcast(FP8X4),
                     rhs_scale=scales[:, rhs],
                     start=(g == 0),
                     stop=(g == PASSES - 1),
                 )
 
-        def in_bank(bank):
-            return bank[:].rearrange("p (j dd h) -> p h dd j", j=VJ, dd=DK)
-
-        def in_output(values):
-            return values.rearrange("p h (dd j) -> p h dd j", j=VJ)
+        def by_head(bank):
+            return bank[:].rearrange("p (d h) -> p h d", h=H)
 
         def hbm(out):
             return out.rearrange("b h (p t) d -> p (b h) t d", t=T)
 
-        g_op = mx_operand("g", VJ * P)
-        v_op = mx_operand("v", VJ * P)
-        qk_op = mx_operand("qk", 2 * P)
         gate = keep.tile([P, H, T, DV], F32, name="gate")
 
-        def gate_pair(a):
+        def silu_pair(a):
             for t in (2 * a, 2 * a + 1):
                 acc = psum.tile([P, BANK], F32, tag="bank", name="g_acc")
-                project(acc[:], t, g_op, VJ * P)
-                nc.scalar.activation(out=in_output(gate[:, :, t, :]), in_=in_bank(acc), func=ACT.Silu)
-            if a % 2 == 1:
-                done = slice(2 * a + 2 - HALF, 2 * a + 2)
-                nc.scalar.activation(out=gate[:, :, done, :], in_=gate[:, :, done, :], func=ACT.Tanh)
-                nc.sync.dma_start(out=hbm(out_1)[:, :, done, :], in_=gate[:, :, done, :])
+                project(acc[:], t, g_op)
+                nc.scalar.activation(out=gate[:, :, t, :], in_=by_head(acc), func=ACT.Silu)
 
-        prepare_weights(g_rows, g_op, VJ, True)
-        prepare_tokens(0, True)
-        for a in range(PAIRS):
-            if a + 1 < PAIRS:
-                prepare_tokens(a + 1, False)
-            else:
-                prepare_weights(v_rows, v_op, VJ, False)
-            gate_pair(a)
-        prepare_weights(qk_rows, qk_op, 2, False)
+        def tanh_half(half):
+            done = slice(half * HALF, (half + 1) * HALF)
+            nc.scalar.activation(out=gate[:, :, done, :], in_=gate[:, :, done, :], func=ACT.Tanh)
+            nc.sync.dma_start(out=hbm(out_1)[:, :, done, :], in_=gate[:, :, done, :])
 
-        qk_out = keep.tile([P, 2, H, T, DK], F32, name="qk_out")
-        v_out = keep.tile([P, H, T, DV], F32, name="v_out")
         N_QK = 2 * 2 * H
-        N_V = 2 * H
-        qk_acc, v_acc, sums, inv = {}, {}, {}, {}
+        qk_acc = {}
+        qk_sq = keep.tile([P, PAIRS, N_QK, DK], F32, name="qk_sq")
+        qk_sums = keep.tile([P, PAIRS * N_QK], F32, name="qk_sums")
+        qk_floored = keep.tile([P, PAIRS * N_QK], F32, name="qk_floored")
+        qk_inv = keep.tile([P, PAIRS * N_QK], F32, name="qk_inv")
+        qk_out = keep.tile([P, 2, H, T, DK], F32, name="qk_out")
 
-        def products(a):
+        def qk_products(a):
             qk_acc[a] = psum.tile([P, BANK], F32, tag="bank", name="qk_acc")
             for i in range(2):
-                project(qk_acc[a][:, i * 2 * P : (i + 1) * 2 * P], 2 * a + i, qk_op, 2 * P)
-            for i in range(2):
-                v_acc[a, i] = psum.tile([P, BANK], F32, tag="bank", name="v_acc")
-                project(v_acc[a, i][:], 2 * a + i, v_op, VJ * P)
-            sums[a] = work.tile([P, N_QK + N_V], F32, name="sums")
+                project(qk_acc[a][:, i * 2 * P : (i + 1) * 2 * P], 2 * a + i, qk_op)
 
         def sum_squares_qk(a):
-            qk_sq = work.tile([P, N_QK, DK], F32, name="qk_sq")
             nc.scalar.activation(
-                out=qk_sq[:].rearrange("p (e h) dd -> p e h dd", h=H),
+                out=qk_sq[:, a].rearrange("p (e h) dd -> p e h dd", h=H),
                 in_=qk_acc[a][:].rearrange("p (e dd h) -> p e h dd", dd=DK, h=H),
                 func=ACT.Square,
             )
             nc.vector.tensor_reduce(
-                out=sums[a][:, 0:N_QK], in_=qk_sq[:], axis=mybir.AxisListType.X, op=ALU.add
+                out=qk_sums[:, a * N_QK : (a + 1) * N_QK],
+                in_=qk_sq[:, a],
+                axis=mybir.AxisListType.X,
+                op=ALU.add,
             )
-
-        def sum_squares_v(a):
-            v_sq = work.tile([P, N_V, DV], F32, name="v_sq")
-            for i in range(2):
-                by_head = v_acc[a, i][:].rearrange("p (m h) -> p h m", h=H)
-                for h in range(H):
-                    e = i * H + h
-                    nc.scalar.activation(
-                        out=v_sq[:, e, :],
-                        in_=by_head[:, h, :],
-                        func=ACT.Square,
-                        accum_out=sums[a][:, N_QK + e : N_QK + e + 1],
-                    )
-
-        def floor_sums(a):
-            floored = work.tile([P, N_QK + N_V], F32, name="floored")
-            nc.vector.tensor_scalar_max(out=floored[:], in0=sums[a][:], scalar1=EPS * EPS)
-            return floored
-
-        def invert_norms(a, floored):
-            inv[a] = work.tile([P, N_QK + N_V], F32, name="inv")
-            nc.scalar.activation(out=inv[a][:], in_=floored[:], func=ACT.Abs_reciprocal_sqrt)
 
         def scale_qk(a):
             both = slice(2 * a, 2 * a + 2)
@@ -253,55 +213,95 @@ def tile_gatedscreeningtile_pa_kernel(
                 nc.vector.tensor_tensor(
                     out=qk_out[:, s, :, both, :],
                     in0=qk_acc[a][:].rearrange("p (i s dd h) -> p s h i dd", i=2, s=2, dd=DK)[:, s],
-                    in1=inv[a][:, 0:N_QK]
+                    in1=qk_inv[:, a * N_QK : (a + 1) * N_QK]
                     .rearrange("p (i s h) -> p s h i", i=2, s=2)[:, s]
                     .unsqueeze(3)
                     .to_broadcast([P, H, 2, DK]),
                     op=ALU.mult,
                 )
 
-        def scale_v(a):
-            for i in range(2):
-                first = N_QK + i * H
-                nc.vector.tensor_tensor(
-                    out=in_output(v_out[:, :, 2 * a + i, :]),
-                    in0=in_bank(v_acc[a, i]),
-                    in1=inv[a][:, first : first + H].unsqueeze(2).unsqueeze(3).to_broadcast([P, H, DK, VJ]),
-                    op=ALU.mult,
-                )
-            both = slice(2 * a, 2 * a + 2)
-            nc.sync.dma_start(out=hbm(out_3)[:, :, both, :], in_=v_out[:, :, both, :])
-
-        def rotate(done):
-            x0 = qk_out[:, :, :, done, 0]
-            x1 = qk_out[:, :, :, done, 1]
-            shape = [P, 2, H, HALF]
-            cos = cos_t[:, :, done].unsqueeze(1).to_broadcast(shape)
-            sin = sin_t[:, :, done].unsqueeze(1).to_broadcast(shape)
-            x0_cos = work.tile(shape, F32, name="x0_cos")
-            x1_sin = work.tile(shape, F32, name="x1_sin")
-            x0_sin = work.tile(shape, F32, name="x0_sin")
-            x1_cos = work.tile(shape, F32, name="x1_cos")
+        def rotate():
+            x0 = qk_out[:, :, :, :, 0]
+            x1 = qk_out[:, :, :, :, 1]
+            shape = [P, 2, H, T]
+            cos = cos_t[:].unsqueeze(1).to_broadcast(shape)
+            sin = sin_t[:].unsqueeze(1).to_broadcast(shape)
+            x0_cos = keep.tile(shape, F32, name="x0_cos")
+            x1_sin = keep.tile(shape, F32, name="x1_sin")
+            x0_sin = keep.tile(shape, F32, name="x0_sin")
+            x1_cos = keep.tile(shape, F32, name="x1_cos")
             nc.vector.tensor_tensor(out=x0_cos[:], in0=x0, in1=cos, op=ALU.mult)
             nc.vector.tensor_tensor(out=x1_sin[:], in0=x1, in1=sin, op=ALU.mult)
             nc.vector.tensor_tensor(out=x0_sin[:], in0=x0, in1=sin, op=ALU.mult)
             nc.vector.tensor_tensor(out=x1_cos[:], in0=x1, in1=cos, op=ALU.mult)
             nc.vector.tensor_tensor(out=x0, in0=x0_cos[:], in1=x1_sin[:], op=ALU.subtract)
             nc.vector.tensor_tensor(out=x1, in0=x0_sin[:], in1=x1_cos[:], op=ALU.add)
-            nc.sync.dma_start(out=hbm(out_0)[:, :, done, :], in_=qk_out[:, 0, :, done, :])
-            nc.sync.dma_start(out=hbm(out_2)[:, :, done, :], in_=qk_out[:, 1, :, done, :])
+            nc.sync.dma_start(out=hbm(out_0), in_=qk_out[:, 0])
+            nc.sync.dma_start(out=hbm(out_2), in_=qk_out[:, 1])
 
-        products(0)
-        sum_squares_qk(0)
+        v_acc = {}
+        v_sq = keep.tile([P, T, H, DV], F32, name="v_sq")
+        v_sums = keep.tile([P, T, H], F32, name="v_sums")
+        v_inv = keep.tile([P, T, H], F32, name="v_inv")
+        v_out = keep.tile([P, H, T, DV], F32, name="v_out")
+
+        def v_products(a):
+            for t in (2 * a, 2 * a + 1):
+                v_acc[t] = psum.tile([P, BANK], F32, tag="bank", name="v_acc")
+                project(v_acc[t][:], t, v_op)
+
+        def invert_norms_v(a):
+            both = slice(2 * a, 2 * a + 2)
+            for t in (2 * a, 2 * a + 1):
+                for h in range(H):
+                    nc.scalar.activation(
+                        out=v_sq[:, t, h, :],
+                        in_=by_head(v_acc[t])[:, h, :],
+                        func=ACT.Square,
+                        accum_out=v_sums[:, t, h : h + 1],
+                    )
+            nc.scalar.activation(out=v_inv[:, both, :], in_=v_sums[:, both, :], func=ACT.Abs_reciprocal_sqrt)
+
+        def scale_v(a):
+            both = slice(2 * a, 2 * a + 2)
+            for t in (2 * a, 2 * a + 1):
+                nc.vector.scalar_tensor_tensor(
+                    out=v_out[:, :, t, :],
+                    in0=v_inv[:, t, :].unsqueeze(2).to_broadcast([P, H, DV]),
+                    scalar=1.0 / EPS,
+                    in1=by_head(v_acc[t]),
+                    op0=ALU.min,
+                    op1=ALU.mult,
+                )
+            nc.sync.dma_start(out=hbm(out_3)[:, :, both, :], in_=v_out[:, :, both, :])
+
+        prepare(0, FIRST)
         for a in range(PAIRS):
-            if a + 1 < PAIRS:
-                products(a + 1)
-            sum_squares_v(a)
-            floored = floor_sums(a)
-            if a + 1 < PAIRS:
-                sum_squares_qk(a + 1)
-            invert_norms(a, floored)
+            silu_pair(a)
+            if a == PAIRS // 2 - 1:
+                sines()
+                tanh_half(0)
+            first = FIRST + a * AHEAD
+            prepare(first, min(AHEAD, len(row_tiles) - first))
+        quantise(len(row_tiles) - 1)
+
+        for a in range(PAIRS):
+            qk_products(a)
+        for a in range(PAIRS // 2):
+            v_products(a)
+        for a in range(PAIRS):
+            sum_squares_qk(a)
+        nc.vector.tensor_scalar_max(out=qk_floored[:], in0=qk_sums[:], scalar1=EPS * EPS)
+        tanh_half(1)
+        nc.scalar.activation(out=qk_inv[:], in_=qk_floored[:], func=ACT.Abs_reciprocal_sqrt)
+
+        for a in range(PAIRS // 2):
+            invert_norms_v(a)
+        for a in range(PAIRS):
             scale_qk(a)
-            if a % 2 == 1:
-                rotate(slice(2 * a + 2 - HALF, 2 * a + 2))
+        rotate()
+        for a in range(PAIRS // 2, PAIRS):
+            v_products(a)
+            invert_norms_v(a)
+        for a in range(PAIRS):
             scale_v(a)

@@ -48,17 +48,22 @@ def tile_gatedscreeningtile_pa_kernel(
         def head_rows(w, first):
             return w.rearrange("(h c) k -> c h k", c=HC)[first : first + DK]
 
-        tok_op = mx_operand("tok", T * P)
+        tok_ops = [mx_operand("tok%d" % t, P) for t in range(T)]
         g_op = mx_operand("g", VJ * P)
         qk_op = mx_operand("qk", 2 * P)
         v_op = mx_operand("v", VJ * P)
         token_tiles = tokens.rearrange("b (p t) k -> t (b p) k", t=T)
         row_tiles = (
             [(g_op, j, head_rows(w_qg, DK + j * DK)) for j in range(VJ)]
-            + [(tok_op, t, token_tiles[t]) for t in range(T)]
+            + [(tok_ops[t], 0, token_tiles[t]) for t in range(T)]
             + [(qk_op, 0, head_rows(w_qg, 0)), (qk_op, 1, head_rows(w_kv, 0))]
             + [(v_op, j, head_rows(w_kv, DK + j * DK)) for j in range(VJ)]
         )
+
+        warm_in = keep.tile([P, 1], F32, name="warm_in")
+        warm_out = keep.tile([P, 1], F32, name="warm_out")
+        nc.vector.memset(warm_in[:], 0.0)
+        nc.scalar.activation(out=warm_out[:], in_=warm_in[:], func=ACT.Silu)
 
         log_window = keep.tile([P, H], BF16, name="log_window")
         nc.scalar.dma_start(out=log_window[:], in_=sm_log.partition_broadcast(P))
@@ -73,8 +78,12 @@ def tile_gatedscreeningtile_pa_kernel(
         nc.gpsimd.iota(pos_int[:], pattern=[[1, T]], base=0, channel_multiplier=T)
         half_pos = keep.tile([P, T], F32, name="half_pos")
         nc.vector.tensor_scalar_mul(out=half_pos[:], in0=pos_int[:], scalar1=0.5)
+        tanh_half = keep.tile([P, H], F32, name="tanh_half")
+        nc.scalar.activation(out=tanh_half[:], in_=log_window[:], func=ACT.Tanh, scale=0.5)
         inv_w = keep.tile([P, H], F32, name="inv_w")
-        nc.scalar.activation(out=inv_w[:], in_=log_window[:], func=ACT.Sigmoid, scale=-1.0)
+        nc.vector.tensor_scalar(
+            out=inv_w[:], in0=tanh_half[:], scalar1=-0.5, scalar2=0.5, op0=ALU.mult, op1=ALU.add
+        )
         window = keep.tile([P, H], F32, name="window")
         nc.vector.reciprocal(out=window[:], in_=inv_w[:])
         below = keep.tile([P, H], F32, name="below")
@@ -133,13 +142,8 @@ def tile_gatedscreeningtile_pa_kernel(
 
         def quantise(n):
             (grouped, codes, scales, columns), j = row_tiles[n][0], row_tiles[n][1]
-            for g in range(PASSES):
-                first = g * columns + j * P
-                nc.vector.quantize_mx(
-                    out=codes[:, first : first + P].bitcast(FP8X4),
-                    scales=scales[:, first : first + P],
-                    in_=grouped[:, 4 * first : 4 * (first + P)],
-                )
+            if (j + 1) * P == columns:
+                nc.vector.quantize_mx(out=codes[:].bitcast(FP8X4), scales=scales[:], in_=grouped[:])
 
         def prepare(first, count):
             for n in range(first, first + count):
@@ -150,12 +154,12 @@ def tile_gatedscreeningtile_pa_kernel(
         def project(acc, t, operand):
             codes, scales, columns = operand[1], operand[2], operand[3]
             for g in range(PASSES):
-                lhs = slice(g * N_TOK + t * P, g * N_TOK + (t + 1) * P)
+                lhs = slice(g * P, (g + 1) * P)
                 rhs = slice(g * columns, (g + 1) * columns)
                 nc.tensor.matmul_mx(
                     out=acc,
-                    lhsT=tok_op[1][:, lhs].bitcast(FP8X4),
-                    lhsT_scale=tok_op[2][:, lhs],
+                    lhsT=tok_ops[t][1][:, lhs].bitcast(FP8X4),
+                    lhsT_scale=tok_ops[t][2][:, lhs],
                     rhs=codes[:, rhs].bitcast(FP8X4),
                     rhs_scale=scales[:, rhs],
                     start=(g == 0),

@@ -78,54 +78,68 @@ def tile_gatedscreeningtile_pa_kernel(
         nc.gpsimd.iota(pos_int[:], pattern=[[1, T]], base=0, channel_multiplier=T)
         half_pos = keep.tile([P, T], F32, name="half_pos")
         nc.vector.tensor_scalar_mul(out=half_pos[:], in0=pos_int[:], scalar1=0.5)
-        tanh_half = keep.tile([P, H], F32, name="tanh_half")
-        nc.scalar.activation(out=tanh_half[:], in_=log_window[:], func=ACT.Tanh, scale=0.5)
+        half_tanh = keep.tile([P, H], F32, name="half_tanh")
         inv_w = keep.tile([P, H], F32, name="inv_w")
-        nc.vector.tensor_scalar(
-            out=inv_w[:], in0=tanh_half[:], scalar1=-0.5, scalar2=0.5, op0=ALU.mult, op1=ALU.add
-        )
         window = keep.tile([P, H], F32, name="window")
-        nc.vector.reciprocal(out=window[:], in_=inv_w[:])
         below = keep.tile([P, H], F32, name="below")
-        nc.vector.tensor_scalar(
-            out=below[:], in0=window[:], scalar1=WINDOW, scalar2=WINDOW, op0=ALU.min, op1=ALU.subtract
-        )
-        root_gamma = keep.tile([P, H], F32, name="root_gamma")
-        nc.scalar.activation(
-            out=root_gamma[:], in_=below[:], func=ACT.Sin, scale=math.pi / (2.0 * WINDOW)
-        )
-        gamma = keep.tile([P, H], F32, name="gamma")
-        nc.gpsimd.tensor_tensor(out=gamma[:], in0=root_gamma[:], in1=root_gamma[:], op=ALU.mult)
-        gamma_by_w = keep.tile([P, H], F32, name="gamma_by_w")
-        nc.gpsimd.tensor_tensor(out=gamma_by_w[:], in0=gamma[:], in1=inv_w[:], op=ALU.mult)
-        turns = keep.tile([P, H, T], F32, name="turns")
-        nc.gpsimd.tensor_tensor(
-            out=turns[:],
-            in0=gamma_by_w[:].unsqueeze(2).to_broadcast([P, H, T]),
-            in1=half_pos[:].unsqueeze(1).to_broadcast([P, H, T]),
-            op=ALU.mult,
-        )
-        whole = keep.tile([P, H, T], F32, name="whole")
-        nc.gpsimd.tensor_scalar(
-            out=whole[:], in0=turns[:], scalar1=ROUND, scalar2=ROUND, op0=ALU.add, op1=ALU.subtract
-        )
         frac = keep.tile([P, H, T], F32, name="frac")
-        nc.gpsimd.tensor_tensor(out=frac[:], in0=turns[:], in1=whole[:], op=ALU.subtract)
-        sin_t = keep.tile([P, H, T], F32, name="sin_t")
-        cos_t = keep.tile([P, H, T], F32, name="cos_t")
+
+        def angles_tanh():
+            nc.scalar.activation(out=half_tanh[:], in_=log_window[:], func=ACT.Tanh, scale=0.5)
+            nc.gpsimd.tensor_scalar(
+                out=inv_w[:], in0=half_tanh[:], scalar1=-0.5, scalar2=0.5, op0=ALU.mult, op1=ALU.add
+            )
+
+        def angles_window():
+            nc.vector.reciprocal(out=window[:], in_=inv_w[:])
+            nc.gpsimd.tensor_scalar(
+                out=below[:], in0=window[:], scalar1=WINDOW, scalar2=WINDOW, op0=ALU.min, op1=ALU.subtract
+            )
+
+        def angles_turns():
+            root_gamma = keep.tile([P, H], F32, name="root_gamma")
+            nc.scalar.activation(
+                out=root_gamma[:], in_=below[:], func=ACT.Sin, scale=math.pi / (2.0 * WINDOW)
+            )
+            gamma = keep.tile([P, H], F32, name="gamma")
+            nc.gpsimd.tensor_tensor(out=gamma[:], in0=root_gamma[:], in1=root_gamma[:], op=ALU.mult)
+            gamma_by_w = keep.tile([P, H], F32, name="gamma_by_w")
+            nc.gpsimd.tensor_tensor(out=gamma_by_w[:], in0=gamma[:], in1=inv_w[:], op=ALU.mult)
+            turns = keep.tile([P, H, T], F32, name="turns")
+            nc.gpsimd.tensor_tensor(
+                out=turns[:],
+                in0=gamma_by_w[:].unsqueeze(2).to_broadcast([P, H, T]),
+                in1=half_pos[:].unsqueeze(1).to_broadcast([P, H, T]),
+                op=ALU.mult,
+            )
+            whole = keep.tile([P, H, T], F32, name="whole")
+            nc.gpsimd.tensor_scalar(
+                out=whole[:], in0=turns[:], scalar1=ROUND, scalar2=ROUND, op0=ALU.add, op1=ALU.subtract
+            )
+            nc.gpsimd.tensor_tensor(out=frac[:], in0=turns[:], in1=whole[:], op=ALU.subtract)
+
+        rot = keep.tile([P, H, T, 2, 2], F32, name="rot")
 
         def sines():
+            sin_t = keep.tile([P, H, T], F32, name="sin_t")
             nc.scalar.activation(out=sin_t[:], in_=frac[:], func=ACT.Sin, scale=2.0 * math.pi)
             half_sin = keep.tile([P, H, T], F32, name="half_sin")
             nc.scalar.activation(out=half_sin[:], in_=frac[:], func=ACT.Sin, scale=math.pi)
+            for j in range(2):
+                nc.gpsimd.tensor_scalar(
+                    out=rot[:, :, :, j, 1 - j], in0=sin_t[:], scalar1=2.0 * j - 1.0, scalar2=0.0,
+                    op0=ALU.mult, op1=ALU.add,
+                )
             half_sq = keep.tile([P, H, T], F32, name="half_sq")
             nc.gpsimd.tensor_tensor(out=half_sq[:], in0=half_sin[:], in1=half_sin[:], op=ALU.mult)
-            nc.gpsimd.tensor_scalar(
-                out=cos_t[:], in0=half_sq[:], scalar1=-2.0, scalar2=1.0, op0=ALU.mult, op1=ALU.add
-            )
+            for j in range(2):
+                nc.gpsimd.tensor_scalar(
+                    out=rot[:, :, :, j, j], in0=half_sq[:], scalar1=-2.0, scalar2=1.0,
+                    op0=ALU.mult, op1=ALU.add,
+                )
 
-        FIRST = VJ + HALF + 1
-        AHEAD = 3
+        FIRST = VJ + 6
+        AHEAD = 2
 
         def flip(n):
             operand, j = row_tiles[n][0], row_tiles[n][1]
@@ -134,7 +148,7 @@ def tile_gatedscreeningtile_pa_kernel(
             for c in range(BANK // P):
                 nc.tensor.transpose(bank[:, c * P : (c + 1) * P], words[:, c * P : (c + 1) * P], ident[:])
             grouped = operand[0][:].bitcast(F32).rearrange("p (g c u) -> p g c u", g=PASSES, u=2)
-            copy = nc.scalar.copy if n < FIRST and n % 2 == 1 else nc.vector.tensor_copy
+            copy = nc.scalar.copy if n < FIRST - 1 else nc.vector.tensor_copy
             copy(
                 out=grouped[:, :, j * P : (j + 1) * P, :],
                 in_=bank[:].rearrange("p (g u r) -> p g r u", g=PASSES, u=2),
@@ -180,9 +194,12 @@ def tile_gatedscreeningtile_pa_kernel(
                 project(acc[:], t, g_op)
                 nc.scalar.activation(out=gate[:, :, t, :], in_=by_head(acc), func=ACT.Silu)
 
-        def tanh_half(half):
+        def tanh_pair(a):
+            both = slice(2 * a, 2 * a + 2)
+            nc.scalar.activation(out=gate[:, :, both, :], in_=gate[:, :, both, :], func=ACT.Tanh)
+
+        def store_gate(half):
             done = slice(half * HALF, (half + 1) * HALF)
-            nc.scalar.activation(out=gate[:, :, done, :], in_=gate[:, :, done, :], func=ACT.Tanh)
             nc.sync.dma_start(out=hbm(out_1)[:, :, done, :], in_=gate[:, :, done, :])
 
         N_QK = 2 * 2 * H
@@ -213,33 +230,27 @@ def tile_gatedscreeningtile_pa_kernel(
 
         def scale_qk(a):
             both = slice(2 * a, 2 * a + 2)
-            for s in range(2):
-                nc.vector.tensor_tensor(
-                    out=qk_out[:, s, :, both, :],
-                    in0=qk_acc[a][:].rearrange("p (i s dd h) -> p s h i dd", i=2, s=2, dd=DK)[:, s],
-                    in1=qk_inv[:, a * N_QK : (a + 1) * N_QK]
-                    .rearrange("p (i s h) -> p s h i", i=2, s=2)[:, s]
-                    .unsqueeze(3)
-                    .to_broadcast([P, H, 2, DK]),
-                    op=ALU.mult,
-                )
+            nc.vector.tensor_tensor(
+                out=qk_out[:, :, :, both, :].rearrange("p s h i dd -> p i s h dd"),
+                in0=qk_acc[a][:].rearrange("p (i s dd h) -> p i s h dd", i=2, s=2, dd=DK),
+                in1=qk_inv[:, a * N_QK : (a + 1) * N_QK]
+                .rearrange("p (i s h) -> p i s h", i=2, s=2)
+                .unsqueeze(4)
+                .to_broadcast([P, 2, 2, H, DK]),
+                op=ALU.mult,
+            )
 
         def rotate():
-            x0 = qk_out[:, :, :, :, 0]
-            x1 = qk_out[:, :, :, :, 1]
-            shape = [P, 2, H, T]
-            cos = cos_t[:].unsqueeze(1).to_broadcast(shape)
-            sin = sin_t[:].unsqueeze(1).to_broadcast(shape)
-            x0_cos = keep.tile(shape, F32, name="x0_cos")
-            x1_sin = keep.tile(shape, F32, name="x1_sin")
-            x0_sin = keep.tile(shape, F32, name="x0_sin")
-            x1_cos = keep.tile(shape, F32, name="x1_cos")
-            nc.vector.tensor_tensor(out=x0_cos[:], in0=x0, in1=cos, op=ALU.mult)
-            nc.vector.tensor_tensor(out=x1_sin[:], in0=x1, in1=sin, op=ALU.mult)
-            nc.vector.tensor_tensor(out=x0_sin[:], in0=x0, in1=sin, op=ALU.mult)
-            nc.vector.tensor_tensor(out=x1_cos[:], in0=x1, in1=cos, op=ALU.mult)
-            nc.vector.tensor_tensor(out=x0, in0=x0_cos[:], in1=x1_sin[:], op=ALU.subtract)
-            nc.vector.tensor_tensor(out=x1, in0=x0_sin[:], in1=x1_cos[:], op=ALU.add)
+            shape = [P, 2, H * T, 2, 2]
+            pairs = qk_out[:].rearrange("p s h t dd -> p s (h t) dd")[:, :, :, 0:2]
+            products = keep.tile(shape, F32, name="products")
+            nc.vector.tensor_tensor(
+                out=products[:],
+                in0=pairs.unsqueeze(3).to_broadcast(shape),
+                in1=rot[:].rearrange("p h t j i -> p (h t) j i").unsqueeze(1).to_broadcast(shape),
+                op=ALU.mult,
+            )
+            nc.vector.tensor_reduce(out=pairs, in_=products[:], axis=mybir.AxisListType.X, op=ALU.add)
             nc.sync.dma_start(out=hbm(out_0), in_=qk_out[:, 0])
             nc.sync.dma_start(out=hbm(out_2), in_=qk_out[:, 1])
 
@@ -279,12 +290,20 @@ def tile_gatedscreeningtile_pa_kernel(
                 )
             nc.sync.dma_start(out=hbm(out_3)[:, :, both, :], in_=v_out[:, :, both, :])
 
-        prepare(0, FIRST)
+        prepare(0, VJ)
+        angles_tanh()
+        prepare(VJ, 2)
+        angles_window()
+        prepare(VJ + 2, 2)
+        angles_turns()
+        prepare(VJ + 4, FIRST - VJ - 4)
         for a in range(PAIRS):
             silu_pair(a)
-            if a == PAIRS // 2 - 1:
+            if a == 1:
                 sines()
-                tanh_half(0)
+            tanh_pair(a)
+            if a % 2 == 1:
+                store_gate(a // 2)
             first = FIRST + a * AHEAD
             prepare(first, min(AHEAD, len(row_tiles) - first))
         quantise(len(row_tiles) - 1)
@@ -296,7 +315,6 @@ def tile_gatedscreeningtile_pa_kernel(
         for a in range(PAIRS):
             sum_squares_qk(a)
         nc.vector.tensor_scalar_max(out=qk_floored[:], in0=qk_sums[:], scalar1=EPS * EPS)
-        tanh_half(1)
         nc.scalar.activation(out=qk_inv[:], in_=qk_floored[:], func=ACT.Abs_reciprocal_sqrt)
 
         for a in range(PAIRS // 2):

@@ -148,7 +148,7 @@ def tile_gatedscreeningtile_pa_kernel(
             for c in range(BANK // P):
                 nc.tensor.transpose(bank[:, c * P : (c + 1) * P], words[:, c * P : (c + 1) * P], ident[:])
             grouped = operand[0][:].bitcast(F32).rearrange("p (g c u) -> p g c u", g=PASSES, u=2)
-            copy = nc.scalar.copy if n < FIRST - 1 else nc.vector.tensor_copy
+            copy = nc.vector.tensor_copy if n in (0, 2) or n >= FIRST - 1 else nc.scalar.copy
             copy(
                 out=grouped[:, :, j * P : (j + 1) * P, :],
                 in_=bank[:].rearrange("p (g u r) -> p g r u", g=PASSES, u=2),
@@ -228,31 +228,30 @@ def tile_gatedscreeningtile_pa_kernel(
                 op=ALU.add,
             )
 
-        def scale_qk(a):
+        def scale_qk(s, a):
             both = slice(2 * a, 2 * a + 2)
             nc.vector.tensor_tensor(
-                out=qk_out[:, :, :, both, :].rearrange("p s h i dd -> p i s h dd"),
-                in0=qk_acc[a][:].rearrange("p (i s dd h) -> p i s h dd", i=2, s=2, dd=DK),
+                out=qk_out[:, s, :, both, :],
+                in0=qk_acc[a][:].rearrange("p (i s dd h) -> p s h i dd", i=2, s=2, dd=DK)[:, s],
                 in1=qk_inv[:, a * N_QK : (a + 1) * N_QK]
-                .rearrange("p (i s h) -> p i s h", i=2, s=2)
-                .unsqueeze(4)
-                .to_broadcast([P, 2, 2, H, DK]),
+                .rearrange("p (i s h) -> p s h i", i=2, s=2)[:, s]
+                .unsqueeze(3)
+                .to_broadcast([P, H, 2, DK]),
                 op=ALU.mult,
             )
 
-        def rotate():
-            shape = [P, 2, H * T, 2, 2]
-            pairs = qk_out[:].rearrange("p s h t dd -> p s (h t) dd")[:, :, :, 0:2]
-            products = keep.tile(shape, F32, name="products")
+        products = keep.tile([P, 2, H * T, 2, 2], F32, name="products")
+
+        def rotate(s, out):
+            pairs = qk_out[:, s].rearrange("p h t dd -> p (h t) dd")[:, :, 0:2]
             nc.vector.tensor_tensor(
-                out=products[:],
-                in0=pairs.unsqueeze(3).to_broadcast(shape),
-                in1=rot[:].rearrange("p h t j i -> p (h t) j i").unsqueeze(1).to_broadcast(shape),
+                out=products[:, s],
+                in0=pairs.unsqueeze(2).to_broadcast([P, H * T, 2, 2]),
+                in1=rot[:].rearrange("p h t j i -> p (h t) j i"),
                 op=ALU.mult,
             )
-            nc.vector.tensor_reduce(out=pairs, in_=products[:], axis=mybir.AxisListType.X, op=ALU.add)
-            nc.sync.dma_start(out=hbm(out_0), in_=qk_out[:, 0])
-            nc.sync.dma_start(out=hbm(out_2), in_=qk_out[:, 1])
+            nc.vector.tensor_reduce(out=pairs, in_=products[:, s], axis=mybir.AxisListType.X, op=ALU.add)
+            nc.sync.dma_start(out=hbm(out), in_=qk_out[:, s])
 
         v_acc = {}
         v_sq = keep.tile([P, T, H, DV], F32, name="v_sq")
@@ -265,30 +264,33 @@ def tile_gatedscreeningtile_pa_kernel(
                 v_acc[t] = psum.tile([P, BANK], F32, tag="bank", name="v_acc")
                 project(v_acc[t][:], t, v_op)
 
-        def invert_norms_v(a):
-            both = slice(2 * a, 2 * a + 2)
-            for t in (2 * a, 2 * a + 1):
-                for h in range(H):
-                    nc.scalar.activation(
-                        out=v_sq[:, t, h, :],
-                        in_=by_head(v_acc[t])[:, h, :],
-                        func=ACT.Square,
-                        accum_out=v_sums[:, t, h : h + 1],
-                    )
-            nc.scalar.activation(out=v_inv[:, both, :], in_=v_sums[:, both, :], func=ACT.Abs_reciprocal_sqrt)
-
-        def scale_v(a):
-            both = slice(2 * a, 2 * a + 2)
-            for t in (2 * a, 2 * a + 1):
-                nc.vector.scalar_tensor_tensor(
-                    out=v_out[:, :, t, :],
-                    in0=v_inv[:, t, :].unsqueeze(2).to_broadcast([P, H, DV]),
-                    scalar=1.0 / EPS,
-                    in1=by_head(v_acc[t]),
-                    op0=ALU.min,
-                    op1=ALU.mult,
+        def sum_squares_v(t):
+            for h in range(H):
+                nc.scalar.activation(
+                    out=v_sq[:, t, h, :],
+                    in_=by_head(v_acc[t])[:, h, :],
+                    func=ACT.Square,
+                    accum_out=v_sums[:, t, h : h + 1],
                 )
-            nc.sync.dma_start(out=hbm(out_3)[:, :, both, :], in_=v_out[:, :, both, :])
+
+        def invert_norms_v(tiles):
+            nc.scalar.activation(out=v_inv[:, tiles, :], in_=v_sums[:, tiles, :], func=ACT.Abs_reciprocal_sqrt)
+
+        def scale_v(t):
+            nc.vector.scalar_tensor_tensor(
+                out=v_out[:, :, t, :],
+                in0=v_inv[:, t, :].unsqueeze(2).to_broadcast([P, H, DV]),
+                scalar=1.0 / EPS,
+                in1=by_head(v_acc[t]),
+                op0=ALU.min,
+                op1=ALU.mult,
+            )
+
+        def store_v(tiles):
+            nc.sync.dma_start(out=hbm(out_3)[:, :, tiles, :], in_=v_out[:, :, tiles, :])
+
+        def pair(a):
+            return slice(2 * a, 2 * a + 2)
 
         prepare(0, VJ)
         angles_tanh()
@@ -318,12 +320,22 @@ def tile_gatedscreeningtile_pa_kernel(
         nc.scalar.activation(out=qk_inv[:], in_=qk_floored[:], func=ACT.Abs_reciprocal_sqrt)
 
         for a in range(PAIRS // 2):
-            invert_norms_v(a)
-        for a in range(PAIRS):
-            scale_qk(a)
-        rotate()
+            sum_squares_v(2 * a)
+            sum_squares_v(2 * a + 1)
+            invert_norms_v(pair(a))
+        for s, out in ((0, out_0), (1, out_2)):
+            for a in range(PAIRS):
+                scale_qk(s, a)
+            rotate(s, out)
         for a in range(PAIRS // 2, PAIRS):
             v_products(a)
-            invert_norms_v(a)
+        sum_squares_v(T - 4)
+        sum_squares_v(T - 3)
+        invert_norms_v(pair(PAIRS - 2))
+        for t in (T - 2, T - 1):
+            sum_squares_v(t)
+            invert_norms_v(slice(t, t + 1))
         for a in range(PAIRS):
-            scale_v(a)
+            scale_v(2 * a)
+            scale_v(2 * a + 1)
+            store_v(pair(a))

@@ -23,6 +23,9 @@ K_PASS = 4 * P
 PASSES = DIM // K_PASS
 BANK = 512
 VJ = DV // DK
+GH = P // DV
+GROUPS = H // GH
+QUAD = BANK // P
 WINDOW = 256.0
 EPS = 1e-12
 ROUND = 1.5 * 2.0**23
@@ -48,6 +51,9 @@ def tile_gatedscreeningtile_pa_kernel(
         def head_rows(w, first):
             return w.rearrange("(h c) k -> c h k", c=HC)[first : first + DK]
 
+        def group_rows(w, group):
+            return w.rearrange("(h c) k -> c h k", c=HC)[DK:HC, group * GH : (group + 1) * GH]
+
         tok_ops = [mx_operand("tok%d" % t, P) for t in range(T)]
         g_op = mx_operand("g", VJ * P)
         qk_op = mx_operand("qk", 2 * P)
@@ -57,7 +63,7 @@ def tile_gatedscreeningtile_pa_kernel(
             [(g_op, j, head_rows(w_qg, DK + j * DK)) for j in range(VJ)]
             + [(tok_ops[t], 0, token_tiles[t]) for t in range(T)]
             + [(qk_op, 0, head_rows(w_qg, 0)), (qk_op, 1, head_rows(w_kv, 0))]
-            + [(v_op, j, head_rows(w_kv, DK + j * DK)) for j in range(VJ)]
+            + [(v_op, group, group_rows(w_kv, group)) for group in range(GROUPS)]
         )
 
         warm_in = keep.tile([P, 1], F32, name="warm_in")
@@ -165,11 +171,11 @@ def tile_gatedscreeningtile_pa_kernel(
                 if n > 0:
                     quantise(n - 1)
 
-        def project(acc, t, operand):
+        def project(acc, t, operand, first=0, count=0):
             codes, scales, columns = operand[1], operand[2], operand[3]
             for g in range(PASSES):
                 lhs = slice(g * P, (g + 1) * P)
-                rhs = slice(g * columns, (g + 1) * columns)
+                rhs = slice(g * columns + first, g * columns + first + (count or columns))
                 nc.tensor.matmul_mx(
                     out=acc,
                     lhsT=tok_ops[t][1][:, lhs].bitcast(FP8X4),
@@ -254,43 +260,54 @@ def tile_gatedscreeningtile_pa_kernel(
             nc.sync.dma_start(out=hbm(out), in_=qk_out[:, s])
 
         v_acc = {}
-        v_sq = keep.tile([P, T, H, DV], F32, name="v_sq")
-        v_sums = keep.tile([P, T, H], F32, name="v_sums")
-        v_inv = keep.tile([P, T, H], F32, name="v_inv")
+        v_sq = keep.tile([P, GROUPS, T, GH, DV], F32, name="v_sq")
+        v_sums = keep.tile([P, GROUPS, T, GH], F32, name="v_sums")
+        v_inv = keep.tile([P, GROUPS, T, GH], F32, name="v_inv")
         v_out = keep.tile([P, H, T, DV], F32, name="v_out")
 
-        def v_products(a):
-            for t in (2 * a, 2 * a + 1):
-                v_acc[t] = psum.tile([P, BANK], F32, tag="bank", name="v_acc")
-                project(v_acc[t][:], t, v_op)
+        def half_tiles(half):
+            return slice(half * QUAD, (half + 1) * QUAD)
 
-        def sum_squares_v(t):
-            for h in range(H):
-                nc.scalar.activation(
-                    out=v_sq[:, t, h, :],
-                    in_=by_head(v_acc[t])[:, h, :],
-                    func=ACT.Square,
-                    accum_out=v_sums[:, t, h : h + 1],
-                )
+        def v_products(group):
+            for half in range(2):
+                v_acc[group, half] = psum.tile([P, BANK], F32, tag="bank", name="v_acc")
+                for i in range(QUAD):
+                    project(
+                        v_acc[group, half][:, i * P : (i + 1) * P], half * QUAD + i, v_op, group * P, P
+                    )
 
-        def invert_norms_v(tiles):
-            nc.scalar.activation(out=v_inv[:, tiles, :], in_=v_sums[:, tiles, :], func=ACT.Abs_reciprocal_sqrt)
+        def by_tile(group, half):
+            return v_acc[group, half][:].rearrange("p (i d e) -> p e i d", i=QUAD, e=GH)
 
-        def scale_v(t):
-            nc.vector.scalar_tensor_tensor(
-                out=v_out[:, :, t, :],
-                in0=v_inv[:, t, :].unsqueeze(2).to_broadcast([P, H, DV]),
-                scalar=1.0 / EPS,
-                in1=by_head(v_acc[t]),
-                op0=ALU.min,
-                op1=ALU.mult,
+        def sum_squares_v(group, half):
+            for i in range(QUAD):
+                for e in range(GH):
+                    nc.scalar.activation(
+                        out=v_sq[:, group, half * QUAD + i, e, :],
+                        in_=by_tile(group, half)[:, e, i, :],
+                        func=ACT.Square,
+                        accum_out=v_sums[:, group, half * QUAD + i, e : e + 1],
+                    )
+
+        def invert_norms_v(group, tiles):
+            nc.scalar.activation(
+                out=v_inv[:, group, tiles, :], in_=v_sums[:, group, tiles, :], func=ACT.Abs_reciprocal_sqrt
             )
 
-        def store_v(tiles):
-            nc.sync.dma_start(out=hbm(out_3)[:, :, tiles, :], in_=v_out[:, :, tiles, :])
+        def scale_v(group, half):
+            for e in range(GH):
+                nc.vector.scalar_tensor_tensor(
+                    out=v_out[:, group * GH + e, half_tiles(half), :],
+                    in0=v_inv[:, group, half_tiles(half), e].unsqueeze(2).to_broadcast([P, QUAD, DV]),
+                    scalar=1.0 / EPS,
+                    in1=by_tile(group, half)[:, e],
+                    op0=ALU.min,
+                    op1=ALU.mult,
+                )
 
-        def pair(a):
-            return slice(2 * a, 2 * a + 2)
+        def store_v(group):
+            heads = slice(group * GH, (group + 1) * GH)
+            nc.sync.dma_start(out=hbm(out_3)[:, heads], in_=v_out[:, heads])
 
         prepare(0, VJ)
         angles_tanh()
@@ -312,30 +329,30 @@ def tile_gatedscreeningtile_pa_kernel(
 
         for a in range(PAIRS):
             qk_products(a)
-        for a in range(PAIRS // 2):
-            v_products(a)
+        for group in range(GROUPS // 2):
+            v_products(group)
         for a in range(PAIRS):
             sum_squares_qk(a)
         nc.vector.tensor_scalar_max(out=qk_floored[:], in0=qk_sums[:], scalar1=EPS * EPS)
         nc.scalar.activation(out=qk_inv[:], in_=qk_floored[:], func=ACT.Abs_reciprocal_sqrt)
 
-        for a in range(PAIRS // 2):
-            sum_squares_v(2 * a)
-            sum_squares_v(2 * a + 1)
-            invert_norms_v(pair(a))
+        for group in range(GROUPS // 2):
+            sum_squares_v(group, 0)
+            sum_squares_v(group, 1)
+            invert_norms_v(group, slice(0, T))
         for s, out in ((0, out_0), (1, out_2)):
             for a in range(PAIRS):
                 scale_qk(s, a)
             rotate(s, out)
-        for a in range(PAIRS // 2, PAIRS):
-            v_products(a)
-        sum_squares_v(T - 4)
-        sum_squares_v(T - 3)
-        invert_norms_v(pair(PAIRS - 2))
-        for t in (T - 2, T - 1):
-            sum_squares_v(t)
-            invert_norms_v(slice(t, t + 1))
-        for a in range(PAIRS):
-            scale_v(2 * a)
-            scale_v(2 * a + 1)
-            store_v(pair(a))
+        for group in range(GROUPS // 2, GROUPS):
+            v_products(group)
+        sum_squares_v(GROUPS - 2, 0)
+        sum_squares_v(GROUPS - 2, 1)
+        invert_norms_v(GROUPS - 2, slice(0, T))
+        for half in range(2):
+            sum_squares_v(GROUPS - 1, half)
+            invert_norms_v(GROUPS - 1, half_tiles(half))
+        for group in range(GROUPS):
+            scale_v(group, 0)
+            scale_v(group, 1)
+            store_v(group)

@@ -144,8 +144,8 @@ def tile_gatedscreeningtile_pa_kernel(
                     op0=ALU.mult, op1=ALU.add,
                 )
 
-        FIRST = VJ + 6
-        AHEAD = 2
+        FIRST = VJ + 4
+        AHEAD = 3
 
         def flip(n):
             operand, j = row_tiles[n][0], row_tiles[n][1]

@@ -250,13 +250,15 @@ def tile_gatedscreeningtile_pa_kernel(
 
         def rotate(s, out):
             pairs = qk_out[:, s].rearrange("p h t dd -> p (h t) dd")[:, :, 0:2]
-            nc.vector.tensor_tensor(
+            nc.gpsimd.tensor_tensor(
                 out=products[:, s],
                 in0=pairs.unsqueeze(2).to_broadcast([P, H * T, 2, 2]),
                 in1=rot[:].rearrange("p h t j i -> p (h t) j i"),
                 op=ALU.mult,
             )
-            nc.vector.tensor_reduce(out=pairs, in_=products[:, s], axis=mybir.AxisListType.X, op=ALU.add)
+            nc.gpsimd.tensor_tensor(
+                out=pairs, in0=products[:, s, :, :, 0], in1=products[:, s, :, :, 1], op=ALU.add
+            )
             nc.sync.dma_start(out=hbm(out), in_=qk_out[:, s])
 
         v_acc = {}
@@ -279,9 +281,9 @@ def tile_gatedscreeningtile_pa_kernel(
         def by_tile(group, half):
             return v_acc[group, half][:].rearrange("p (i d e) -> p e i d", i=QUAD, e=GH)
 
-        def sum_squares_v(group, half):
-            for i in range(QUAD):
-                for e in range(GH):
+        def sum_squares_v(group, half, heads=(0, 1)):
+            for e in heads:
+                for i in range(QUAD):
                     nc.scalar.activation(
                         out=v_sq[:, group, half * QUAD + i, e, :],
                         in_=by_tile(group, half)[:, e, i, :],
@@ -289,24 +291,25 @@ def tile_gatedscreeningtile_pa_kernel(
                         accum_out=v_sums[:, group, half * QUAD + i, e : e + 1],
                     )
 
-        def invert_norms_v(group, tiles):
+        def invert_norms_v(group, tiles, heads=slice(0, GH)):
             nc.scalar.activation(
-                out=v_inv[:, group, tiles, :], in_=v_sums[:, group, tiles, :], func=ACT.Abs_reciprocal_sqrt
+                out=v_inv[:, group, tiles, heads],
+                in_=v_sums[:, group, tiles, heads],
+                func=ACT.Abs_reciprocal_sqrt,
             )
 
-        def scale_v(group, half):
-            for e in range(GH):
-                nc.vector.scalar_tensor_tensor(
-                    out=v_out[:, group * GH + e, half_tiles(half), :],
-                    in0=v_inv[:, group, half_tiles(half), e].unsqueeze(2).to_broadcast([P, QUAD, DV]),
-                    scalar=1.0 / EPS,
-                    in1=by_tile(group, half)[:, e],
-                    op0=ALU.min,
-                    op1=ALU.mult,
-                )
+        def scale_v(group, half, e):
+            nc.vector.scalar_tensor_tensor(
+                out=v_out[:, group * GH + e, half_tiles(half), :],
+                in0=v_inv[:, group, half_tiles(half), e].unsqueeze(2).to_broadcast([P, QUAD, DV]),
+                scalar=1.0 / EPS,
+                in1=by_tile(group, half)[:, e],
+                op0=ALU.min,
+                op1=ALU.mult,
+            )
 
-        def store_v(group):
-            heads = slice(group * GH, (group + 1) * GH)
+        def store_v(first, count):
+            heads = slice(first, first + count)
             nc.sync.dma_start(out=hbm(out_3)[:, heads], in_=v_out[:, heads])
 
         prepare(0, VJ)
@@ -336,6 +339,7 @@ def tile_gatedscreeningtile_pa_kernel(
         nc.vector.tensor_scalar_max(out=qk_floored[:], in0=qk_sums[:], scalar1=EPS * EPS)
         nc.scalar.activation(out=qk_inv[:], in_=qk_floored[:], func=ACT.Abs_reciprocal_sqrt)
 
+        LAST = GROUPS - 1
         for group in range(GROUPS // 2):
             sum_squares_v(group, 0)
             sum_squares_v(group, 1)
@@ -346,13 +350,21 @@ def tile_gatedscreeningtile_pa_kernel(
             rotate(s, out)
         for group in range(GROUPS // 2, GROUPS):
             v_products(group)
-        sum_squares_v(GROUPS - 2, 0)
-        sum_squares_v(GROUPS - 2, 1)
-        invert_norms_v(GROUPS - 2, slice(0, T))
+        sum_squares_v(LAST - 1, 0)
+        sum_squares_v(LAST - 1, 1)
+        invert_norms_v(LAST - 1, slice(0, T))
+        sum_squares_v(LAST, 0, (0,))
+        sum_squares_v(LAST, 1, (0,))
+        invert_norms_v(LAST, slice(0, T), slice(0, 1))
         for half in range(2):
-            sum_squares_v(GROUPS - 1, half)
-            invert_norms_v(GROUPS - 1, half_tiles(half))
-        for group in range(GROUPS):
-            scale_v(group, 0)
-            scale_v(group, 1)
-            store_v(group)
+            sum_squares_v(LAST, half, (1,))
+            invert_norms_v(LAST, half_tiles(half), slice(1, 2))
+        for group in range(LAST):
+            for half in range(2):
+                for e in range(GH):
+                    scale_v(group, half, e)
+            store_v(group * GH, GH)
+        for e in range(GH):
+            for half in range(2):
+                scale_v(LAST, half, e)
+            store_v(LAST * GH + e, 1)

@@ -71,8 +71,11 @@ def tile_gatedscreeningtile_pa_kernel(
         nc.vector.memset(warm_in[:], 0.0)
         nc.scalar.activation(out=warm_out[:], in_=warm_in[:], func=ACT.Silu)
 
-        log_window = keep.tile([P, H], BF16, name="log_window")
-        nc.scalar.dma_start(out=log_window[:], in_=sm_log.partition_broadcast(P))
+        log_row = keep.tile([P, H], BF16, name="log_row")
+        nc.gpsimd.memset(log_row[:], 0.0)
+        nc.scalar.dma_start(out=log_row[0:1, :], in_=sm_log.unsqueeze(0))
+        ones = keep.tile([P, P], BF16, name="ones")
+        nc.gpsimd.memset(ones[:], 1.0)
         rows = keep.tile([P, len(row_tiles) * DIM], BF16, name="rows")
         for n in range(len(row_tiles)):
             nc.sync.dma_start(out=rows[:, n * DIM : (n + 1) * DIM], in_=row_tiles[n][2])
@@ -91,7 +94,9 @@ def tile_gatedscreeningtile_pa_kernel(
         frac = keep.tile([P, H, T], F32, name="frac")
 
         def angles_tanh():
-            nc.scalar.activation(out=half_tanh[:], in_=log_window[:], func=ACT.Tanh, scale=0.5)
+            log_window = psum.tile([P, BANK], F32, tag="bank", name="log_window")
+            nc.tensor.matmul(out=log_window[:, 0:H], lhsT=ones[:], rhs=log_row[:], start=True, stop=True)
+            nc.scalar.activation(out=half_tanh[:], in_=log_window[:, 0:H], func=ACT.Tanh, scale=0.5)
             nc.gpsimd.tensor_scalar(
                 out=inv_w[:], in0=half_tanh[:], scalar1=-0.5, scalar2=0.5, op0=ALU.mult, op1=ALU.add
             )

@@ -76,6 +76,16 @@ def tile_gatedscreeningtile_pa_kernel(
         nc.scalar.dma_start(out=log_row[0:1, :], in_=sm_log.unsqueeze(0))
         ones = keep.tile([P, P], BF16, name="ones")
         nc.gpsimd.memset(ones[:], 1.0)
+
+        zeros = keep.tile([P, BANK], BF16, name="zeros")
+        nc.gpsimd.memset(zeros[:], 0.0)
+        idle_bank = psum.tile([P, BANK], F32, tag="bank", name="idle_bank")
+
+        def keep_busy(count):
+            for i in range(count):
+                nc.tensor.matmul(out=idle_bank[:], lhsT=ones[:], rhs=zeros[:], start=True, stop=True)
+
+        keep_busy(4)
         rows = keep.tile([P, len(row_tiles) * DIM], BF16, name="rows")
         for n in range(len(row_tiles)):
             nc.sync.dma_start(out=rows[:, n * DIM : (n + 1) * DIM], in_=row_tiles[n][2])
@@ -173,6 +183,8 @@ def tile_gatedscreeningtile_pa_kernel(
         def prepare(first, count):
             for n in range(first, first + count):
                 flip(n)
+                if n < FIRST - 2:
+                    keep_busy(1)
                 if n > 0:
                     quantise(n - 1)
 

@@ -55,12 +55,12 @@ def tile_gatedscreeningtile_pa_kernel(
             return w.rearrange("(h c) k -> c h k", c=HC)[DK:HC, group * GH : (group + 1) * GH]
 
         tok_ops = [mx_operand("tok%d" % t, P) for t in range(T)]
-        g_op = mx_operand("g", VJ * P)
+        g_ops = [mx_operand("g%d" % i, 2 * P) for i in range(VJ // 2)]
         qk_op = mx_operand("qk", 2 * P)
         v_op = mx_operand("v", VJ * P)
         token_tiles = tokens.rearrange("b (p t) k -> t (b p) k", t=T)
         row_tiles = (
-            [(g_op, j, head_rows(w_qg, DK + j * DK)) for j in range(VJ)]
+            [(g_ops[j // 2], j % 2, head_rows(w_qg, DK + j * DK)) for j in range(VJ)]
             + [(tok_ops[t], 0, token_tiles[t]) for t in range(T)]
             + [(qk_op, 0, head_rows(w_qg, 0)), (qk_op, 1, head_rows(w_kv, 0))]
             + [(v_op, group, group_rows(w_kv, group)) for group in range(GROUPS)]
@@ -214,7 +214,8 @@ def tile_gatedscreeningtile_pa_kernel(
         def silu_pair(a):
             for t in (2 * a, 2 * a + 1):
                 acc = psum.tile([P, BANK], F32, tag="bank", name="g_acc")
-                project(acc[:], t, g_op)
+                for i in range(VJ // 2):
+                    project(acc[:, i * 2 * P : (i + 1) * 2 * P], t, g_ops[i])
                 nc.scalar.activation(out=gate[:, :, t, :], in_=by_head(acc), func=ACT.Silu)
 
         def tanh_pair(a):

import math
from contextlib import ExitStack

import concourse.masks as masks
import concourse.mybir as mybir

F32 = mybir.dt.float32
BF16 = mybir.dt.bfloat16
I32 = mybir.dt.int32
U32 = mybir.dt.uint32
U8 = mybir.dt.uint8
FP8X4 = mybir.dt.float8_e4m3fn_x4
ACT = mybir.ActivationFunctionType
ALU = mybir.AluOpType

P = 128
N_TOK, DIM, H, DK, DV = 1024, 1024, 8, 16, 64
HC = DK + DV
T = N_TOK // P
PAIRS = T // 2
HALF = T // 2
K_PASS = 4 * P
PASSES = DIM // K_PASS
BANK = 512
VJ = DV // DK
GH = P // DV
GROUPS = H // GH
QUAD = BANK // P
WINDOW = 256.0
EPS = 1e-12
ROUND = 1.5 * 2.0**23

FLOPS = 2 * N_TOK * DIM * 2 * H * HC


def tile_gatedscreeningtile_pa_kernel(
    tc, tokens, w_qg, w_kv, sm_log, out_0, out_1, out_2, out_3
):
    nc = tc.nc
    with ExitStack() as ctx:
        keep = ctx.enter_context(tc.tile_pool(name="keep", bufs=1))
        psum = ctx.enter_context(tc.psum_pool(name="psum", bufs=8))
        ctx.enter_context(tc.manual_schedule())

        def mx_operand(name, columns):
            grouped = keep.tile([P, PASSES * columns * 4], BF16, name=name + "_grouped", align_bytes=64)
            codes = keep.tile([P, PASSES * columns], U32, name=name + "_codes", align_bytes=64)
            scales = keep.tile([P, PASSES * columns], U8, name=name + "_scales", align_bytes=64)
            return grouped, codes, scales, columns

        def head_rows(w, first):
            return w.rearrange("(h c) k -> c h k", c=HC)[first : first + DK]

        def group_rows(w, group):
            return w.rearrange("(h c) k -> c h k", c=HC)[DK:HC, group * GH : (group + 1) * GH]

        tok_ops = [mx_operand("tok%d" % t, P) for t in range(T)]
        g_ops = [mx_operand("g%d" % i, 2 * P) for i in range(VJ // 2)]
        qk_op = mx_operand("qk", 2 * P)
        v_op = mx_operand("v", VJ * P)
        token_tiles = tokens.rearrange("b (p t) k -> t (b p) k", t=T)
        row_tiles = (
            [(g_ops[j // 2], j % 2, head_rows(w_qg, DK + j * DK)) for j in range(VJ)]
            + [(tok_ops[t], 0, token_tiles[t]) for t in range(T)]
            + [(qk_op, 0, head_rows(w_qg, 0)), (qk_op, 1, head_rows(w_kv, 0))]
            + [(v_op, group, group_rows(w_kv, group)) for group in range(GROUPS)]
        )

        warm_in = keep.tile([P, 1], F32, name="warm_in")
        warm_out = keep.tile([P, 1], F32, name="warm_out")
        nc.vector.memset(warm_in[:], 0.0)
        nc.scalar.activation(out=warm_out[:], in_=warm_in[:], func=ACT.Silu)

        log_row = keep.tile([P, H], BF16, name="log_row")
        nc.gpsimd.memset(log_row[:], 0.0)
        nc.scalar.dma_start(out=log_row[0:1, :], in_=sm_log.unsqueeze(0))
        ones = keep.tile([P, P], BF16, name="ones")
        nc.gpsimd.memset(ones[:], 1.0)

        zeros = keep.tile([P, BANK], BF16, name="zeros")
        nc.gpsimd.memset(zeros[:], 0.0)
        idle_bank = psum.tile([P, BANK], F32, tag="bank", name="idle_bank")

        def keep_busy(count):
            for i in range(count):
                nc.tensor.matmul(out=idle_bank[:], lhsT=ones[:], rhs=zeros[:], start=True, stop=True)

        keep_busy(4)
        rows = keep.tile([P, len(row_tiles) * DIM], BF16, name="rows")
        for n in range(len(row_tiles)):
            nc.sync.dma_start(out=rows[:, n * DIM : (n + 1) * DIM], in_=row_tiles[n][2])

        ident = keep.tile([P, P], F32, name="ident")
        masks.make_identity(nc, ident[:])

        pos_int = keep.tile([P, T], I32, name="pos_int")
        nc.gpsimd.iota(pos_int[:], pattern=[[1, T]], base=0, channel_multiplier=T)
        half_pos = keep.tile([P, T], F32, name="half_pos")
        nc.vector.tensor_scalar_mul(out=half_pos[:], in0=pos_int[:], scalar1=0.5)
        half_tanh = keep.tile([P, H], F32, name="half_tanh")
        inv_w = keep.tile([P, H], F32, name="inv_w")
        window = keep.tile([P, H], F32, name="window")
        below = keep.tile([P, H], F32, name="below")
        frac = keep.tile([P, H, T], F32, name="frac")

        def angles_tanh():
            log_window = psum.tile([P, BANK], F32, tag="bank", name="log_window")
            nc.tensor.matmul(out=log_window[:, 0:H], lhsT=ones[:], rhs=log_row[:], start=True, stop=True)
            nc.scalar.activation(out=half_tanh[:], in_=log_window[:, 0:H], func=ACT.Tanh, scale=0.5)
            nc.gpsimd.tensor_scalar(
                out=inv_w[:], in0=half_tanh[:], scalar1=-0.5, scalar2=0.5, op0=ALU.mult, op1=ALU.add
            )

        def angles_window():
            nc.vector.reciprocal(out=window[:], in_=inv_w[:])
            nc.gpsimd.tensor_scalar(
                out=below[:], in0=window[:], scalar1=WINDOW, scalar2=WINDOW, op0=ALU.min, op1=ALU.subtract
            )

        def angles_turns():
            root_gamma = keep.tile([P, H], F32, name="root_gamma")
            nc.scalar.activation(
                out=root_gamma[:], in_=below[:], func=ACT.Sin, scale=math.pi / (2.0 * WINDOW)
            )
            gamma = keep.tile([P, H], F32, name="gamma")
            nc.gpsimd.tensor_tensor(out=gamma[:], in0=root_gamma[:], in1=root_gamma[:], op=ALU.mult)
            gamma_by_w = keep.tile([P, H], F32, name="gamma_by_w")
            nc.gpsimd.tensor_tensor(out=gamma_by_w[:], in0=gamma[:], in1=inv_w[:], op=ALU.mult)
            turns = keep.tile([P, H, T], F32, name="turns")
            nc.gpsimd.tensor_tensor(
                out=turns[:],
                in0=gamma_by_w[:].unsqueeze(2).to_broadcast([P, H, T]),
                in1=half_pos[:].unsqueeze(1).to_broadcast([P, H, T]),
                op=ALU.mult,
            )
            whole = keep.tile([P, H, T], F32, name="whole")
            nc.gpsimd.tensor_scalar(
                out=whole[:], in0=turns[:], scalar1=ROUND, scalar2=ROUND, op0=ALU.add, op1=ALU.subtract
            )
            nc.gpsimd.tensor_tensor(out=frac[:], in0=turns[:], in1=whole[:], op=ALU.subtract)

        rot = keep.tile([P, H, T, 2, 2], F32, name="rot")

        def sines():
            sin_t = keep.tile([P, H, T], F32, name="sin_t")
            nc.scalar.activation(out=sin_t[:], in_=frac[:], func=ACT.Sin, scale=2.0 * math.pi)
            half_sin = keep.tile([P, H, T], F32, name="half_sin")
            nc.scalar.activation(out=half_sin[:], in_=frac[:], func=ACT.Sin, scale=math.pi)
            for j in range(2):
                nc.gpsimd.tensor_scalar(
                    out=rot[:, :, :, j, 1 - j], in0=sin_t[:], scalar1=2.0 * j - 1.0, scalar2=0.0,
                    op0=ALU.mult, op1=ALU.add,
                )
            half_sq = keep.tile([P, H, T], F32, name="half_sq")
            nc.gpsimd.tensor_tensor(out=half_sq[:], in0=half_sin[:], in1=half_sin[:], op=ALU.mult)
            for j in range(2):
                nc.gpsimd.tensor_scalar(
                    out=rot[:, :, :, j, j], in0=half_sq[:], scalar1=-2.0, scalar2=1.0,
                    op0=ALU.mult, op1=ALU.add,
                )

        FIRST = VJ + 4
        AHEAD = 3

        def flip(n):
            operand, j = row_tiles[n][0], row_tiles[n][1]
            words = rows[:].bitcast(F32)[:, n * BANK : (n + 1) * BANK]
            bank = psum.tile([P, BANK], F32, tag="bank", name="flipped")
            for c in range(BANK // P):
                nc.tensor.transpose(bank[:, c * P : (c + 1) * P], words[:, c * P : (c + 1) * P], ident[:])
            grouped = operand[0][:].bitcast(F32).rearrange("p (g c u) -> p g c u", g=PASSES, u=2)
            copy = nc.vector.tensor_copy if n in (0, 2) or n >= FIRST - 1 else nc.scalar.copy
            copy(
                out=grouped[:, :, j * P : (j + 1) * P, :],
                in_=bank[:].rearrange("p (g u r) -> p g r u", g=PASSES, u=2),
            )

        def quantise(n):
            (grouped, codes, scales, columns), j = row_tiles[n][0], row_tiles[n][1]
            if (j + 1) * P == columns:
                nc.vector.quantize_mx(out=codes[:].bitcast(FP8X4), scales=scales[:], in_=grouped[:])

        def prepare(first, count):
            for n in range(first, first + count):
                flip(n)
                if n < FIRST - 2:
                    keep_busy(1)
                if n > 0:
                    quantise(n - 1)

        def project(acc, t, operand, first=0, count=0):
            codes, scales, columns = operand[1], operand[2], operand[3]
            for g in range(PASSES):
                lhs = slice(g * P, (g + 1) * P)
                rhs = slice(g * columns + first, g * columns + first + (count or columns))
                nc.tensor.matmul_mx(
                    out=acc,
                    lhsT=tok_ops[t][1][:, lhs].bitcast(FP8X4),
                    lhsT_scale=tok_ops[t][2][:, lhs],
                    rhs=codes[:, rhs].bitcast(FP8X4),
                    rhs_scale=scales[:, rhs],
                    start=(g == 0),
                    stop=(g == PASSES - 1),
                )

        def by_head(bank):
            return bank[:].rearrange("p (d h) -> p h d", h=H)

        def hbm(out):
            return out.rearrange("b h (p t) d -> p (b h) t d", t=T)

        gate = keep.tile([P, H, T, DV], F32, name="gate")

        def silu_pair(a):
            for t in (2 * a, 2 * a + 1):
                acc = psum.tile([P, BANK], F32, tag="bank", name="g_acc")
                for i in range(VJ // 2):
                    project(acc[:, i * 2 * P : (i + 1) * 2 * P], t, g_ops[i])
                nc.scalar.activation(out=gate[:, :, t, :], in_=by_head(acc), func=ACT.Silu)

        def tanh_pair(a):
            both = slice(2 * a, 2 * a + 2)
            nc.scalar.activation(out=gate[:, :, both, :], in_=gate[:, :, both, :], func=ACT.Tanh)

        def store_gate(half):
            done = slice(half * HALF, (half + 1) * HALF)
            nc.sync.dma_start(out=hbm(out_1)[:, :, done, :], in_=gate[:, :, done, :])

        N_QK = 2 * 2 * H
        qk_acc = {}
        qk_sq = keep.tile([P, PAIRS, N_QK, DK], F32, name="qk_sq")
        qk_sums = keep.tile([P, PAIRS * N_QK], F32, name="qk_sums")
        qk_floored = keep.tile([P, PAIRS * N_QK], F32, name="qk_floored")
        qk_inv = keep.tile([P, PAIRS * N_QK], F32, name="qk_inv")
        qk_out = keep.tile([P, 2, H, T, DK], F32, name="qk_out")

        def qk_products(a):
            qk_acc[a] = psum.tile([P, BANK], F32, tag="bank", name="qk_acc")
            for i in range(2):
                project(qk_acc[a][:, i * 2 * P : (i + 1) * 2 * P], 2 * a + i, qk_op)

        def sum_squares_qk(a):
            nc.scalar.activation(
                out=qk_sq[:, a].rearrange("p (e h) dd -> p e h dd", h=H),
                in_=qk_acc[a][:].rearrange("p (e dd h) -> p e h dd", dd=DK, h=H),
                func=ACT.Square,
            )
            nc.vector.tensor_reduce(
                out=qk_sums[:, a * N_QK : (a + 1) * N_QK],
                in_=qk_sq[:, a],
                axis=mybir.AxisListType.X,
                op=ALU.add,
            )

        def scale_qk(s, a):
            both = slice(2 * a, 2 * a + 2)
            nc.vector.tensor_tensor(
                out=qk_out[:, s, :, both, :],
                in0=qk_acc[a][:].rearrange("p (i s dd h) -> p s h i dd", i=2, s=2, dd=DK)[:, s],
                in1=qk_inv[:, a * N_QK : (a + 1) * N_QK]
                .rearrange("p (i s h) -> p s h i", i=2, s=2)[:, s]
                .unsqueeze(3)
                .to_broadcast([P, H, 2, DK]),
                op=ALU.mult,
            )

        products = keep.tile([P, 2, H * T, 2, 2], F32, name="products")

        def rotate(s, out):
            pairs = qk_out[:, s].rearrange("p h t dd -> p (h t) dd")[:, :, 0:2]
            nc.gpsimd.tensor_tensor(
                out=products[:, s],
                in0=pairs.unsqueeze(2).to_broadcast([P, H * T, 2, 2]),
                in1=rot[:].rearrange("p h t j i -> p (h t) j i"),
                op=ALU.mult,
            )
            nc.gpsimd.tensor_tensor(
                out=pairs, in0=products[:, s, :, :, 0], in1=products[:, s, :, :, 1], op=ALU.add
            )
            nc.sync.dma_start(out=hbm(out), in_=qk_out[:, s])

        v_acc = {}
        v_sq = keep.tile([P, GROUPS, T, GH, DV], F32, name="v_sq")
        v_sums = keep.tile([P, GROUPS, T, GH], F32, name="v_sums")
        v_inv = keep.tile([P, GROUPS, T, GH], F32, name="v_inv")
        v_out = keep.tile([P, H, T, DV], F32, name="v_out")

        def half_tiles(half):
            return slice(half * QUAD, (half + 1) * QUAD)

        def v_products(group):
            for half in range(2):
                v_acc[group, half] = psum.tile([P, BANK], F32, tag="bank", name="v_acc")
                for i in range(QUAD):
                    project(
                        v_acc[group, half][:, i * P : (i + 1) * P], half * QUAD + i, v_op, group * P, P
                    )

        def by_tile(group, half):
            return v_acc[group, half][:].rearrange("p (i d e) -> p e i d", i=QUAD, e=GH)

        def sum_squares_v(group, half, heads=(0, 1)):
            for e in heads:
                for i in range(QUAD):
                    nc.scalar.activation(
                        out=v_sq[:, group, half * QUAD + i, e, :],
                        in_=by_tile(group, half)[:, e, i, :],
                        func=ACT.Square,
                        accum_out=v_sums[:, group, half * QUAD + i, e : e + 1],
                    )

        def invert_norms_v(group, tiles, heads=slice(0, GH)):
            nc.scalar.activation(
                out=v_inv[:, group, tiles, heads],
                in_=v_sums[:, group, tiles, heads],
                func=ACT.Abs_reciprocal_sqrt,
            )

        def scale_v(group, half, e):
            nc.vector.scalar_tensor_tensor(
                out=v_out[:, group * GH + e, half_tiles(half), :],
                in0=v_inv[:, group, half_tiles(half), e].unsqueeze(2).to_broadcast([P, QUAD, DV]),
                scalar=1.0 / EPS,
                in1=by_tile(group, half)[:, e],
                op0=ALU.min,
                op1=ALU.mult,
            )

        def store_v(first, count):
            heads = slice(first, first + count)
            nc.sync.dma_start(out=hbm(out_3)[:, heads], in_=v_out[:, heads])

        prepare(0, VJ)
        angles_tanh()
        prepare(VJ, 2)
        angles_window()
        prepare(VJ + 2, 2)
        angles_turns()
        prepare(VJ + 4, FIRST - VJ - 4)
        for a in range(PAIRS):
            silu_pair(a)
            if a == 1:
                sines()
            tanh_pair(a)
            if a % 2 == 1:
                store_gate(a // 2)
            first = FIRST + a * AHEAD
            prepare(first, min(AHEAD, len(row_tiles) - first))
        quantise(len(row_tiles) - 1)

        for a in range(PAIRS):
            qk_products(a)
        for group in range(GROUPS // 2):
            v_products(group)
        for a in range(PAIRS):
            sum_squares_qk(a)
        nc.vector.tensor_scalar_max(out=qk_floored[:], in0=qk_sums[:], scalar1=EPS * EPS)
        nc.scalar.activation(out=qk_inv[:], in_=qk_floored[:], func=ACT.Abs_reciprocal_sqrt)

        LAST = GROUPS - 1
        for group in range(GROUPS // 2):
            sum_squares_v(group, 0)
            sum_squares_v(group, 1)
            invert_norms_v(group, slice(0, T))
        for s, out in ((0, out_0), (1, out_2)):
            for a in range(PAIRS):
                scale_qk(s, a)
            rotate(s, out)
        for group in range(GROUPS // 2, GROUPS):
            v_products(group)
        sum_squares_v(LAST - 1, 0)
        sum_squares_v(LAST - 1, 1)
        invert_norms_v(LAST - 1, slice(0, T))
        sum_squares_v(LAST, 0, (0,))
        sum_squares_v(LAST, 1, (0,))
        invert_norms_v(LAST, slice(0, T), slice(0, 1))
        for half in range(2):
            sum_squares_v(LAST, half, (1,))
            invert_norms_v(LAST, half_tiles(half), slice(1, 2))
        for group in range(LAST):
            for half in range(2):
                for e in range(GH):
                    scale_v(group, half, e)
            store_v(group * GH, GH)
        for e in range(GH):
            for half in range(2):
                scale_v(LAST, half, e)
            store_v(LAST * GH + e, 1)
